import numpy as np
import ml_dtypes


def mxq(x, axis, fmt="e4m3"):
    dtype, down = {"e4m3": (ml_dtypes.float8_e4m3fn, 7), "e5m2": (ml_dtypes.float8_e5m2, 14)}[fmt]
    v = np.moveaxis(np.asarray(x, np.float32).astype(ml_dtypes.bfloat16).astype(np.float64), axis, -1)
    blocks = v.reshape(v.shape[:-1] + (-1, 32))
    amax = np.abs(blocks).max(-1, keepdims=True)
    byte = np.maximum(np.where(amax > 0, np.frexp(amax)[1] - 1 + 127, 0) - down, 1)
    scale = np.exp2(byte - 127.0)
    codes = (blocks / scale).astype(np.float32).astype(dtype).astype(np.float64)
    return np.moveaxis((codes * scale).reshape(v.shape), -1, axis)


WIDE = False


def mx_kscale(k):
    if not WIDE:
        return np.ones(k)
    levels = np.array([10, -10, 5, -5, 0])
    a = np.random.permutation(np.resize(levels, k // 512 * 4)).reshape(k // 512, 4)
    idx = np.arange(k)
    return np.exp2(a[idx // 512, idx % 128 // 32])


BF16 = ml_dtypes.bfloat16


def bf(x):
    return np.asarray(x, np.float32).astype(BF16)


def f64(x):
    return np.asarray(x).astype(np.float64)


B, S, H, HS, D = 128, 8, 8, 128, 1024
M = H * HS
FORGET_BIAS = 1.0


def sigmoid(v):
    return 1.0 / (1.0 + np.exp(-v))


def setup_inputs():
    s, t = mx_kscale(M), mx_kscale(D)
    n = np.random.standard_normal
    return {
        'inputs': bf(n((B, D)) * t),
        'h_state': bf(n((B, S, M)) * s),
        'm_state': bf(n((B, S, M))),
        'mem_att': bf(n((B, S, M)) * 2.0),
        'W_g': bf(n((M, M)) * 0.5 / np.sqrt(M)), 'b_g': bf(n(M) * 0.5),
        'W_wf': bf(n((D, M)) / np.sqrt(D) / t[:, None]),
        'W_wi': bf(n((D, M)) / np.sqrt(D) / t[:, None]),
        'W_wo': bf(n((D, M)) / np.sqrt(D) / t[:, None]),
        'W_uf': bf(n((M, M)) / np.sqrt(M) / s[:, None]), 'b_uf': bf(n(M)),
        'W_ui': bf(n((M, M)) / np.sqrt(M) / s[:, None]), 'b_ui': bf(n(M)),
        'W_uo': bf(n((M, M)) / np.sqrt(M) / s[:, None]), 'b_uo': bf(n(M)),
    }


def reference(inputs, h_state, m_state, mem_att, W_g, b_g, W_wf, W_wi, W_wo, W_uf, b_uf, W_ui, b_ui, W_uo, b_uo):
    m = f64(m_state)
    p = f64(mem_att)
    xq = mxq(f64(inputs), 1, 'e4m3')
    hq = mxq(f64(h_state), 2, 'e4m3')
    memory_proposal = ((mxq(p, 2, 'e4m3') @ mxq(f64(W_g), 0, 'e4m3')) + f64(b_g)) + p
    forget_gate = sigmoid((hq @ mxq(f64(W_uf), 0, 'e4m3')) + f64(b_uf) + (xq @ mxq(f64(W_wf), 0, 'e4m3'))[:, None, :])
    input_gate = sigmoid((hq @ mxq(f64(W_ui), 0, 'e4m3')) + f64(b_ui) + (xq @ mxq(f64(W_wi), 0, 'e4m3'))[:, None, :])
    output_gate = sigmoid((hq @ mxq(f64(W_uo), 0, 'e4m3')) + f64(b_uo) + (xq @ mxq(f64(W_wo), 0, 'e4m3'))[:, None, :])
    new_memories = sigmoid(m * forget_gate + FORGET_BIAS) + memory_proposal * sigmoid(input_gate)
    new_hidden = np.tanh(m) * sigmoid(output_gate)
    return new_memories, new_hidden

@@ -1,0 +1,200 @@
+from contextlib import ExitStack
+
+import concourse.mybir as mybir
+from concourse.masks import make_identity
+
+F32 = mybir.dt.float32
+BF16 = mybir.dt.bfloat16
+U32 = mybir.dt.uint32
+U8 = mybir.dt.uint8
+FP8X4 = mybir.dt.float8_e4m3fn_x4
+ACT = mybir.ActivationFunctionType
+ALU = mybir.AluOpType
+
+P = 128
+SLOTS = 8
+WIDTH = 1024
+PACK = 4
+K_PASS = P * PACK
+PASSES = WIDTH // K_PASS
+N_TILE = 512
+HALVES = WIDTH // N_TILE
+QUANT_COLS = 2048
+
+FLOPS = 2 * P * SLOTS * WIDTH * WIDTH * 4 + 2 * P * WIDTH * WIDTH * 3
+
+
+def quantise_rows(nc, pools, ident, src, n_slots, codes, scales):
+    rows = n_slots * P
+    src_words = src.bitcast(F32)
+    grouped = pools["big"].tile([P, PASSES * rows * PACK], BF16, tag="big", align_bytes=64, name="grouped_rows")
+    grouped_words = grouped[:].bitcast(F32).rearrange("q (g s b u) -> q g s b u", g=PASSES, s=n_slots, b=P, u=2)
+    for s in range(n_slots):
+        flipped = pools["flip"].tile([P, PASSES * 2 * P], F32, tag="flip", name="flipped")
+        for a in range(PASSES * 2):
+            nc.tensor.transpose(
+                flipped[:, a * P : (a + 1) * P],
+                src_words[:, (s * PASSES * 2 + a) * P : (s * PASSES * 2 + a + 1) * P],
+                ident,
+            )
+        nc.scalar.copy(
+            out=grouped_words[:, :, s, :, :],
+            in_=flipped[:].rearrange("q (g u b) -> q g b u", g=PASSES, u=2, b=P),
+        )
+    step = min(QUANT_COLS, rows * PACK)
+    for start in range(0, PASSES * rows * PACK, step):
+        nc.vector.quantize_mx(
+            out=codes[:, start // PACK : (start + step) // PACK].bitcast(FP8X4),
+            scales=scales[:, start // PACK : (start + step) // PACK],
+            in_=grouped[:, start : start + step],
+        )
+
+
+def quantise_weight(nc, pools, weight, name):
+    raw = pools["big"].tile([P, PASSES * PACK * WIDTH], BF16, tag="big", align_bytes=64, name="raw_" + name)
+    nc.sync.dma_start(
+        out=raw[:].rearrange("q (a r) -> q a r", a=PASSES * 2),
+        in_=weight.rearrange("(a q e) n -> q a (e n)", a=PASSES * 2, q=P, e=2),
+    )
+    raw_rows = raw[:].rearrange("q (g t n) -> q g t n", g=PASSES, t=PACK, n=WIDTH)
+    codes = pools["wq"].tile([P, PASSES * WIDTH], U32, tag="w_codes", align_bytes=64, name="codes_" + name)
+    scales = pools["wq"].tile([P, PASSES * WIDTH], U8, tag="w_scales", align_bytes=64, name="scales_" + name)
+    for g in range(PASSES):
+        for c in range(HALVES):
+            grouped = pools["group"].tile([P, N_TILE * PACK], BF16, tag="grouped", align_bytes=64, name="grouped_w")
+            dst = grouped[:].rearrange("q (c i t) -> q c t i", i=4, t=PACK)
+            src = raw_rows[:, g, :, c * N_TILE : (c + 1) * N_TILE].rearrange("q t (c i) -> q c t i", i=4)
+            if (g * HALVES + c) % 4 == 0:
+                nc.vector.tensor_copy(out=dst, in_=src)
+            else:
+                nc.scalar.copy(out=dst, in_=src)
+            cols = slice(g * WIDTH + c * N_TILE, g * WIDTH + (c + 1) * N_TILE)
+            nc.vector.quantize_mx(out=codes[:, cols].bitcast(FP8X4), scales=scales[:, cols], in_=grouped[:])
+    return codes, scales
+
+
+def product(nc, pools, rows_q, row_tile, weight_q, c):
+    row_codes, row_scales, rows = rows_q
+    w_codes, w_scales = weight_q
+    acc = pools["acc"].tile([P, N_TILE], F32, tag="acc", name="acc")
+    for g in range(PASSES):
+        m_cols = slice(g * rows + row_tile * P, g * rows + (row_tile + 1) * P)
+        n_cols = slice(g * WIDTH + c * N_TILE, g * WIDTH + (c + 1) * N_TILE)
+        nc.tensor.matmul_mx(
+            out=acc[:],
+            lhsT=row_codes[:, m_cols].bitcast(FP8X4),
+            lhsT_scale=row_scales[:, m_cols],
+            rhs=w_codes[:, n_cols].bitcast(FP8X4),
+            rhs_scale=w_scales[:, n_cols],
+            start=(g == 0),
+            stop=(g == PASSES - 1),
+        )
+    return acc
+
+
+def input_term(nc, pools, x_q, weight_q, bias, name):
+    bias_rows = pools["bias"].tile([P, WIDTH], BF16, tag="bias", name="bias_" + name)
+    nc.sync.dma_start(out=bias_rows[:], in_=bias.partition_broadcast(P))
+    term = pools["term"].tile([P, WIDTH], F32, tag="term", name="term_" + name)
+    for c in range(HALVES):
+        cols = slice(c * N_TILE, (c + 1) * N_TILE)
+        acc = product(nc, pools, x_q, 0, weight_q, c)
+        nc.vector.tensor_tensor(out=term[:, cols], in0=acc[:], in1=bias_rows[:, cols], op=ALU.add)
+    return term
+
+
+def gate(nc, pools, h_q, s, weight_q, term):
+    g_tile = pools["work"].tile([P, WIDTH], F32, tag="gate", name="gate")
+    for c in range(HALVES):
+        cols = slice(c * N_TILE, (c + 1) * N_TILE)
+        acc = product(nc, pools, h_q, s, weight_q, c)
+        nc.vector.tensor_tensor(out=g_tile[:, cols], in0=acc[:], in1=term[:, cols], op=ALU.add)
+    nc.scalar.activation(out=g_tile[:], in_=g_tile[:], func=ACT.Sigmoid)
+    return g_tile
+
+
+def tile_relationalmemorycorecell_pa_kernel(
+    tc, inputs, h_state, m_state, mem_att, W_g, b_g, W_wf, W_wi, W_wo, W_uf, b_uf, W_ui, b_ui, W_uo, b_uo, out_0, out_1
+):
+    nc = tc.nc
+    with ExitStack() as ctx:
+        pools = {
+            "const": ctx.enter_context(tc.tile_pool(name="const", bufs=1)),
+            "big": ctx.enter_context(tc.tile_pool(name="big", bufs=4)),
+            "group": ctx.enter_context(tc.tile_pool(name="group", bufs=3)),
+            "wq": ctx.enter_context(tc.tile_pool(name="wq", bufs=3)),
+            "bias": ctx.enter_context(tc.tile_pool(name="bias", bufs=2)),
+            "term": ctx.enter_context(tc.tile_pool(name="term", bufs=2)),
+            "work": ctx.enter_context(tc.tile_pool(name="work", bufs=4)),
+            "flip": ctx.enter_context(tc.psum_pool(name="flip", bufs=2)),
+            "acc": ctx.enter_context(tc.psum_pool(name="acc", bufs=6)),
+        }
+        const = pools["const"]
+        ident = const.tile([P, P], F32, name="ident")
+        make_identity(nc, ident[:])
+
+        rows_all = SLOTS * P
+        p_codes = const.tile([P, PASSES * rows_all], U32, align_bytes=64, name="p_codes")
+        p_scales = const.tile([P, PASSES * rows_all], U8, align_bytes=64, name="p_scales")
+        h_codes = const.tile([P, PASSES * rows_all], U32, align_bytes=64, name="h_codes")
+        h_scales = const.tile([P, PASSES * rows_all], U8, align_bytes=64, name="h_scales")
+        x_codes = const.tile([P, PASSES * P], U32, align_bytes=64, name="x_codes")
+        x_scales = const.tile([P, PASSES * P], U8, align_bytes=64, name="x_scales")
+        p_q = (p_codes, p_scales, rows_all)
+        h_q = (h_codes, h_scales, rows_all)
+        x_q = (x_codes, x_scales, P)
+
+        p_sb = pools["big"].tile([P, SLOTS * WIDTH], BF16, tag="big", align_bytes=64, name="p_sb")
+        nc.sync.dma_start(out=p_sb[:], in_=mem_att.rearrange("b s n -> b (s n)"))
+        wg_q = quantise_weight(nc, pools, W_g, "g")
+        bg_rows = pools["bias"].tile([P, WIDTH], BF16, tag="bias", name="bias_g")
+        nc.sync.dma_start(out=bg_rows[:], in_=b_g.partition_broadcast(P))
+        quantise_rows(nc, pools, ident[:], p_sb[:], SLOTS, p_codes, p_scales)
+        prop = const.tile([P, SLOTS, WIDTH], F32, name="prop")
+        p_slots = p_sb[:].rearrange("b (s n) -> b s n", s=SLOTS)
+        for s in range(0, SLOTS, 2):
+            nc.vector.tensor_tensor(
+                out=prop[:, s : s + 2, :],
+                in0=p_slots[:, s : s + 2, :],
+                in1=bg_rows[:].unsqueeze(1).to_broadcast([P, 2, WIDTH]),
+                op=ALU.add,
+            )
+        for s in range(SLOTS):
+            for c in range(HALVES):
+                cols = slice(c * N_TILE, (c + 1) * N_TILE)
+                acc = product(nc, pools, p_q, s, wg_q, c)
+                nc.vector.tensor_tensor(out=prop[:, s, cols], in0=acc[:], in1=prop[:, s, cols], op=ALU.add)
+
+        x_sb = const.tile([P, WIDTH], BF16, name="x_sb")
+        nc.sync.dma_start(out=x_sb[:], in_=inputs)
+        h_sb = pools["big"].tile([P, SLOTS * WIDTH], BF16, tag="big", align_bytes=64, name="h_sb")
+        nc.sync.dma_start(out=h_sb[:], in_=h_state.rearrange("b s n -> b (s n)"))
+        quantise_rows(nc, pools, ident[:], x_sb[:], 1, x_codes, x_scales)
+        term_i = input_term(nc, pools, x_q, quantise_weight(nc, pools, W_wi, "wi"), b_ui, "i")
+        quantise_rows(nc, pools, ident[:], h_sb[:], SLOTS, h_codes, h_scales)
+        wui_q = quantise_weight(nc, pools, W_ui, "ui")
+        for s in range(SLOTS):
+            i_gate = gate(nc, pools, h_q, s, wui_q, term_i)
+            nc.scalar.activation(out=i_gate[:], in_=i_gate[:], func=ACT.Sigmoid)
+            nc.vector.tensor_tensor(out=prop[:, s, :], in0=prop[:, s, :], in1=i_gate[:], op=ALU.mult)
+
+        m_sb = const.tile([P, SLOTS, WIDTH], BF16, name="m_sb")
+        nc.sync.dma_start(out=m_sb[:], in_=m_state)
+        term_f = input_term(nc, pools, x_q, quantise_weight(nc, pools, W_wf, "wf"), b_uf, "f")
+        wuf_q = quantise_weight(nc, pools, W_uf, "uf")
+        for s in range(SLOTS):
+            f_gate = gate(nc, pools, h_q, s, wuf_q, term_f)
+            nc.vector.tensor_tensor(out=f_gate[:], in0=f_gate[:], in1=m_sb[:, s, :], op=ALU.mult)
+            nc.scalar.activation(out=f_gate[:], in_=f_gate[:], func=ACT.Sigmoid, bias=1.0)
+            nc.vector.tensor_tensor(out=f_gate[:], in0=f_gate[:], in1=prop[:, s, :], op=ALU.add)
+            nc.gpsimd.dma_start(out=out_0[:, s, :], in_=f_gate[:])
+
+        term_o = input_term(nc, pools, x_q, quantise_weight(nc, pools, W_wo, "wo"), b_uo, "o")
+        wuo_q = quantise_weight(nc, pools, W_uo, "uo")
+        for s in range(SLOTS):
+            o_gate = gate(nc, pools, h_q, s, wuo_q, term_o)
+            nc.scalar.activation(out=o_gate[:], in_=o_gate[:], func=ACT.Sigmoid)
+            tanh_m = pools["work"].tile([P, WIDTH], F32, tag="tanh", bufs=2, name="tanh_m")
+            nc.scalar.activation(out=tanh_m[:], in_=m_sb[:, s, :], func=ACT.Tanh)
+            nc.vector.tensor_tensor(out=o_gate[:], in0=o_gate[:], in1=tanh_m[:], op=ALU.mult)
+            nc.gpsimd.dma_start(out=out_1[:, s, :], in_=o_gate[:])

@@ -15,186 +15,298 @@ P = 128
 SLOTS = 8
 WIDTH = 1024
 PACK = 4
-K_PASS = P * PACK
-PASSES = WIDTH // K_PASS
-N_TILE = 512
-HALVES = WIDTH // N_TILE
-QUANT_COLS = 2048
+PASSES = WIDTH // (P * PACK)
+K_TILES = WIDTH // P
+GROUP_SLOTS = 4
+ROWS = GROUP_SLOTS * P
+ROW_GROUPS = SLOTS // GROUP_SLOTS
+UNITS = 2
+BLOCK = UNITS * P
+BLOCKS = WIDTH // BLOCK
 
 FLOPS = 2 * P * SLOTS * WIDTH * WIDTH * 4 + 2 * P * WIDTH * WIDTH * 3
 
-
-def quantise_rows(nc, pools, ident, src, n_slots, codes, scales):
-    rows = n_slots * P
-    src_words = src.bitcast(F32)
-    grouped = pools["big"].tile([P, PASSES * rows * PACK], BF16, tag="big", align_bytes=64, name="grouped_rows")
-    grouped_words = grouped[:].bitcast(F32).rearrange("q (g s b u) -> q g s b u", g=PASSES, s=n_slots, b=P, u=2)
-    for s in range(n_slots):
-        flipped = pools["flip"].tile([P, PASSES * 2 * P], F32, tag="flip", name="flipped")
-        for a in range(PASSES * 2):
-            nc.tensor.transpose(
-                flipped[:, a * P : (a + 1) * P],
-                src_words[:, (s * PASSES * 2 + a) * P : (s * PASSES * 2 + a + 1) * P],
-                ident,
-            )
-        nc.scalar.copy(
-            out=grouped_words[:, :, s, :, :],
-            in_=flipped[:].rearrange("q (g u b) -> q g b u", g=PASSES, u=2, b=P),
-        )
-    step = min(QUANT_COLS, rows * PACK)
-    for start in range(0, PASSES * rows * PACK, step):
-        nc.vector.quantize_mx(
-            out=codes[:, start // PACK : (start + step) // PACK].bitcast(FP8X4),
-            scales=scales[:, start // PACK : (start + step) // PACK],
-            in_=grouped[:, start : start + step],
-        )
-
-
-def quantise_weight(nc, pools, weight, name):
-    raw = pools["big"].tile([P, PASSES * PACK * WIDTH], BF16, tag="big", align_bytes=64, name="raw_" + name)
-    nc.sync.dma_start(
-        out=raw[:].rearrange("q (a r) -> q a r", a=PASSES * 2),
-        in_=weight.rearrange("(a q e) n -> q a (e n)", a=PASSES * 2, q=P, e=2),
-    )
-    raw_rows = raw[:].rearrange("q (g t n) -> q g t n", g=PASSES, t=PACK, n=WIDTH)
-    codes = pools["wq"].tile([P, PASSES * WIDTH], U32, tag="w_codes", align_bytes=64, name="codes_" + name)
-    scales = pools["wq"].tile([P, PASSES * WIDTH], U8, tag="w_scales", align_bytes=64, name="scales_" + name)
-    for g in range(PASSES):
-        for c in range(HALVES):
-            grouped = pools["group"].tile([P, N_TILE * PACK], BF16, tag="grouped", align_bytes=64, name="grouped_w")
-            dst = grouped[:].rearrange("q (c i t) -> q c t i", i=4, t=PACK)
-            src = raw_rows[:, g, :, c * N_TILE : (c + 1) * N_TILE].rearrange("q t (c i) -> q c t i", i=4)
-            if (g * HALVES + c) % 4 == 0:
-                nc.vector.tensor_copy(out=dst, in_=src)
-            else:
-                nc.scalar.copy(out=dst, in_=src)
-            cols = slice(g * WIDTH + c * N_TILE, g * WIDTH + (c + 1) * N_TILE)
-            nc.vector.quantize_mx(out=codes[:, cols].bitcast(FP8X4), scales=scales[:, cols], in_=grouped[:])
-    return codes, scales
-
-
-def product(nc, pools, rows_q, row_tile, weight_q, c):
-    row_codes, row_scales, rows = rows_q
-    w_codes, w_scales = weight_q
-    acc = pools["acc"].tile([P, N_TILE], F32, tag="acc", name="acc")
-    for g in range(PASSES):
-        m_cols = slice(g * rows + row_tile * P, g * rows + (row_tile + 1) * P)
-        n_cols = slice(g * WIDTH + c * N_TILE, g * WIDTH + (c + 1) * N_TILE)
-        nc.tensor.matmul_mx(
-            out=acc[:],
-            lhsT=row_codes[:, m_cols].bitcast(FP8X4),
-            lhsT_scale=row_scales[:, m_cols],
-            rhs=w_codes[:, n_cols].bitcast(FP8X4),
-            rhs_scale=w_scales[:, n_cols],
-            start=(g == 0),
-            stop=(g == PASSES - 1),
-        )
-    return acc
-
-
-def input_term(nc, pools, x_q, weight_q, bias, name):
-    bias_rows = pools["bias"].tile([P, WIDTH], BF16, tag="bias", name="bias_" + name)
-    nc.sync.dma_start(out=bias_rows[:], in_=bias.partition_broadcast(P))
-    term = pools["term"].tile([P, WIDTH], F32, tag="term", name="term_" + name)
-    for c in range(HALVES):
-        cols = slice(c * N_TILE, (c + 1) * N_TILE)
-        acc = product(nc, pools, x_q, 0, weight_q, c)
-        nc.vector.tensor_tensor(out=term[:, cols], in0=acc[:], in1=bias_rows[:, cols], op=ALU.add)
-    return term
-
-
-def gate(nc, pools, h_q, s, weight_q, term):
-    g_tile = pools["work"].tile([P, WIDTH], F32, tag="gate", name="gate")
-    for c in range(HALVES):
-        cols = slice(c * N_TILE, (c + 1) * N_TILE)
-        acc = product(nc, pools, h_q, s, weight_q, c)
-        nc.vector.tensor_tensor(out=g_tile[:, cols], in0=acc[:], in1=term[:, cols], op=ALU.add)
-    nc.scalar.activation(out=g_tile[:], in_=g_tile[:], func=ACT.Sigmoid)
-    return g_tile
+PHASE_WEIGHTS = {"o": ("uo", "wo"), "f": ("uf", "wf"), "ig": ("ui", "wi", "g")}
+BIAS_ORDER = ("g", "f", "i", "o")
+OUT_BUFS = {"o": 3, "f": 7}
 
 
 def tile_relationalmemorycorecell_pa_kernel(
     tc, inputs, h_state, m_state, mem_att, W_g, b_g, W_wf, W_wi, W_wo, W_uf, b_uf, W_ui, b_ui, W_uo, b_uo, out_0, out_1
 ):
     nc = tc.nc
+    weight_of = {"g": W_g, "wf": W_wf, "wi": W_wi, "wo": W_wo, "uf": W_uf, "ui": W_ui, "uo": W_uo}
+    bias_of = {"g": b_g, "f": b_uf, "i": b_ui, "o": b_uo}
+    rows_of = {"h": h_state, "p": mem_att}
+
+    phases = []
+    for jp in range(BLOCKS + 1):
+        if jp < BLOCKS:
+            phases.extend([("o", jp), ("f", jp)])
+        if jp >= 1:
+            phases.append(("ig", jp - 1))
+    steps = [(kind, jp, r) for (kind, jp) in phases for r in range(ROW_GROUPS)]
+
     with ExitStack() as ctx:
-        pools = {
-            "const": ctx.enter_context(tc.tile_pool(name="const", bufs=1)),
-            "big": ctx.enter_context(tc.tile_pool(name="big", bufs=4)),
-            "group": ctx.enter_context(tc.tile_pool(name="group", bufs=3)),
-            "wq": ctx.enter_context(tc.tile_pool(name="wq", bufs=3)),
-            "bias": ctx.enter_context(tc.tile_pool(name="bias", bufs=2)),
-            "term": ctx.enter_context(tc.tile_pool(name="term", bufs=2)),
-            "work": ctx.enter_context(tc.tile_pool(name="work", bufs=4)),
-            "flip": ctx.enter_context(tc.psum_pool(name="flip", bufs=2)),
-            "acc": ctx.enter_context(tc.psum_pool(name="acc", bufs=6)),
-        }
-        const = pools["const"]
-        ident = const.tile([P, P], F32, name="ident")
-        make_identity(nc, ident[:])
+        const = ctx.enter_context(tc.tile_pool(name="const", bufs=1))
+        rows_pool = ctx.enter_context(tc.tile_pool(name="rows", bufs=2))
+        w_raw_pool = ctx.enter_context(tc.tile_pool(name="w_raw", bufs=8))
+        w_grouped_pool = ctx.enter_context(tc.tile_pool(name="w_grouped", bufs=4))
+        w_q_pool = ctx.enter_context(tc.tile_pool(name="w_q", bufs=9))
+        work = ctx.enter_context(tc.tile_pool(name="work", bufs=3))
+        acc_pool = ctx.enter_context(tc.psum_pool(name="acc", bufs=4))
+        back_pool = ctx.enter_context(tc.psum_pool(name="back", bufs=4))
 
-        rows_all = SLOTS * P
-        p_codes = const.tile([P, PASSES * rows_all], U32, align_bytes=64, name="p_codes")
-        p_scales = const.tile([P, PASSES * rows_all], U8, align_bytes=64, name="p_scales")
-        h_codes = const.tile([P, PASSES * rows_all], U32, align_bytes=64, name="h_codes")
-        h_scales = const.tile([P, PASSES * rows_all], U8, align_bytes=64, name="h_scales")
-        x_codes = const.tile([P, PASSES * P], U32, align_bytes=64, name="x_codes")
-        x_scales = const.tile([P, PASSES * P], U8, align_bytes=64, name="x_scales")
-        p_q = (p_codes, p_scales, rows_all)
-        h_q = (h_codes, h_scales, rows_all)
-        x_q = (x_codes, x_scales, P)
-
-        p_sb = pools["big"].tile([P, SLOTS * WIDTH], BF16, tag="big", align_bytes=64, name="p_sb")
-        nc.sync.dma_start(out=p_sb[:], in_=mem_att.rearrange("b s n -> b (s n)"))
-        wg_q = quantise_weight(nc, pools, W_g, "g")
-        bg_rows = pools["bias"].tile([P, WIDTH], BF16, tag="bias", name="bias_g")
-        nc.sync.dma_start(out=bg_rows[:], in_=b_g.partition_broadcast(P))
-        quantise_rows(nc, pools, ident[:], p_sb[:], SLOTS, p_codes, p_scales)
-        prop = const.tile([P, SLOTS, WIDTH], F32, name="prop")
-        p_slots = p_sb[:].rearrange("b (s n) -> b s n", s=SLOTS)
-        for s in range(0, SLOTS, 2):
-            nc.vector.tensor_tensor(
-                out=prop[:, s : s + 2, :],
-                in0=p_slots[:, s : s + 2, :],
-                in1=bg_rows[:].unsqueeze(1).to_broadcast([P, 2, WIDTH]),
-                op=ALU.add,
-            )
-        for s in range(SLOTS):
-            for c in range(HALVES):
-                cols = slice(c * N_TILE, (c + 1) * N_TILE)
-                acc = product(nc, pools, p_q, s, wg_q, c)
-                nc.vector.tensor_tensor(out=prop[:, s, cols], in0=acc[:], in1=prop[:, s, cols], op=ALU.add)
+        ident_f = const.tile([P, P], F32, name="ident_f")
+        make_identity(nc, ident_f[:])
+        ident_b = const.tile([P, P], BF16, name="ident_b")
+        make_identity(nc, ident_b[:])
+        ctx.enter_context(tc.manual_schedule())
 
         x_sb = const.tile([P, WIDTH], BF16, name="x_sb")
+        rows_raw = {}
+        w_raw = {}
+        m_blocks = {}
+
+        def load_rows(name, r):
+            raw = rows_pool.tile([P, GROUP_SLOTS * WIDTH], BF16, tag="rows_raw", name="raw_" + name)
+            src = rows_of[name][:, r * GROUP_SLOTS : (r + 1) * GROUP_SLOTS, :]
+            nc.sync.dma_start(out=raw[:], in_=src.rearrange("b s n -> b (s n)"))
+            rows_raw[(name, r)] = raw
+
+        def load_weight(name, jp):
+            raw = w_raw_pool.tile([P, K_TILES, BLOCK], BF16, tag="w_raw", name="raw_" + name)
+            src = weight_of[name][:, jp * BLOCK : (jp + 1) * BLOCK]
+            nc.sync.dma_start(out=raw[:], in_=src.rearrange("(a c) n -> c a n", c=P))
+            w_raw[(name, jp)] = raw
+
         nc.sync.dma_start(out=x_sb[:], in_=inputs)
-        h_sb = pools["big"].tile([P, SLOTS * WIDTH], BF16, tag="big", align_bytes=64, name="h_sb")
-        nc.sync.dma_start(out=h_sb[:], in_=h_state.rearrange("b s n -> b (s n)"))
-        quantise_rows(nc, pools, ident[:], x_sb[:], 1, x_codes, x_scales)
-        term_i = input_term(nc, pools, x_q, quantise_weight(nc, pools, W_wi, "wi"), b_ui, "i")
-        quantise_rows(nc, pools, ident[:], h_sb[:], SLOTS, h_codes, h_scales)
-        wui_q = quantise_weight(nc, pools, W_ui, "ui")
-        for s in range(SLOTS):
-            i_gate = gate(nc, pools, h_q, s, wui_q, term_i)
-            nc.scalar.activation(out=i_gate[:], in_=i_gate[:], func=ACT.Sigmoid)
-            nc.vector.tensor_tensor(out=prop[:, s, :], in0=prop[:, s, :], in1=i_gate[:], op=ALU.mult)
+        load_rows("h", 0)
+        for kind, jp in phases:
+            if (kind, jp) == ("ig", 0):
+                load_rows("p", 0)
+                load_rows("p", 1)
+            for name in PHASE_WEIGHTS[kind]:
+                load_weight(name, jp)
+            if (kind, jp) == ("o", 0):
+                load_rows("h", 1)
+            if kind == "o":
+                m_block = const.tile([P, SLOTS, BLOCK], BF16, name="m_block%d" % jp)
+                nc.sync.dma_start(out=m_block[:], in_=m_state[:, :, jp * BLOCK : (jp + 1) * BLOCK])
+                m_blocks[jp] = m_block
 
-        m_sb = const.tile([P, SLOTS, WIDTH], BF16, name="m_sb")
-        nc.sync.dma_start(out=m_sb[:], in_=m_state)
-        term_f = input_term(nc, pools, x_q, quantise_weight(nc, pools, W_wf, "wf"), b_uf, "f")
-        wuf_q = quantise_weight(nc, pools, W_uf, "uf")
-        for s in range(SLOTS):
-            f_gate = gate(nc, pools, h_q, s, wuf_q, term_f)
-            nc.vector.tensor_tensor(out=f_gate[:], in0=f_gate[:], in1=m_sb[:, s, :], op=ALU.mult)
-            nc.scalar.activation(out=f_gate[:], in_=f_gate[:], func=ACT.Sigmoid, bias=1.0)
-            nc.vector.tensor_tensor(out=f_gate[:], in0=f_gate[:], in1=prop[:, s, :], op=ALU.add)
-            nc.gpsimd.dma_start(out=out_0[:, s, :], in_=f_gate[:])
+        bias_rows = const.tile([P, P], BF16, name="bias_rows")
+        nc.vector.memset(bias_rows[:], 0.0)
+        for k, key in enumerate(BIAS_ORDER):
+            nc.scalar.dma_start(
+                out=bias_rows[k * K_TILES : (k + 1) * K_TILES, :],
+                in_=bias_of[key].rearrange("(j c) -> j c", c=P),
+            )
+        bias_flipped = back_pool.tile([P, WIDTH], BF16, tag="back", name="bias_flipped")
+        nc.tensor.transpose(bias_flipped[:, 0:P], bias_rows[:], ident_b[:])
+        bias_cols = const.tile([P, P], F32, name="bias_cols")
+        nc.vector.tensor_copy(out=bias_cols[:], in_=bias_flipped[:, 0:P])
 
-        term_o = input_term(nc, pools, x_q, quantise_weight(nc, pools, W_wo, "wo"), b_uo, "o")
-        wuo_q = quantise_weight(nc, pools, W_uo, "uo")
-        for s in range(SLOTS):
-            o_gate = gate(nc, pools, h_q, s, wuo_q, term_o)
-            nc.scalar.activation(out=o_gate[:], in_=o_gate[:], func=ACT.Sigmoid)
-            tanh_m = pools["work"].tile([P, WIDTH], F32, tag="tanh", bufs=2, name="tanh_m")
-            nc.scalar.activation(out=tanh_m[:], in_=m_sb[:, s, :], func=ACT.Tanh)
-            nc.vector.tensor_tensor(out=o_gate[:], in0=o_gate[:], in1=tanh_m[:], op=ALU.mult)
-            nc.gpsimd.dma_start(out=out_1[:, s, :], in_=o_gate[:])
+        def bias_col(key, jp, u):
+            col = BIAS_ORDER.index(key) * K_TILES + jp * UNITS + u
+            return bias_cols[:, col : col + 1]
+
+        rows_q = {}
+        w_q = {}
+        p_grouped = {}
+
+        def flip(raw_cols):
+            flipped = back_pool.tile([P, WIDTH], BF16, tag="back", name="flipped")
+            for a in range(K_TILES):
+                nc.tensor.transpose(flipped[:, a * P : (a + 1) * P], raw_cols[:, a * P : (a + 1) * P], ident_b[:])
+            return flipped[:].rearrange("c (g t b) -> c g b t", g=PASSES, t=PACK, b=P)
+
+        def new_grouped_rows(name):
+            grouped = rows_pool.tile([P, PASSES * ROWS * PACK], BF16, tag="rows_grouped", align_bytes=64, name=name)
+            view = grouped[:].rearrange("c (g s b t) -> c g s b t", g=PASSES, s=GROUP_SLOTS, b=P, t=PACK)
+            return grouped, view
+
+        def quantise_rows(key, grouped):
+            codes = const.tile([P, PASSES * ROWS], U32, align_bytes=64, name="codes_%s%d" % key)
+            scales = const.tile([P, PASSES * ROWS], U8, align_bytes=64, name="scales_%s%d" % key)
+            nc.vector.quantize_mx(out=codes[:].bitcast(FP8X4), scales=scales[:], in_=grouped[:])
+            rows_q[key] = (codes, scales)
+
+        def group_rows(name, r):
+            grouped, view = new_grouped_rows("grouped_" + name)
+            raw = rows_raw[(name, r)]
+            for s in range(GROUP_SLOTS):
+                flipped = flip(raw[:, s * WIDTH : (s + 1) * WIDTH])
+                copy = nc.scalar.copy if s % 2 == 0 else nc.vector.tensor_copy
+                copy(out=view[:, :, s, :, :], in_=flipped)
+            return grouped
+
+        def group_weight(name, jp, copy):
+            raw = w_raw[(name, jp)]
+            grouped = w_grouped_pool.tile([P, PASSES * BLOCK * PACK], BF16, tag="w_grouped", align_bytes=64, name="grouped_w")
+            for g in range(PASSES):
+                dst = grouped[:, g * BLOCK * PACK : (g + 1) * BLOCK * PACK]
+                copy(
+                    out=dst.rearrange("c (n i t) -> c n t i", i=4, t=PACK),
+                    in_=raw[:, g * PACK : (g + 1) * PACK, :].rearrange("c t (n i) -> c n t i", i=4),
+                )
+            return grouped
+
+        def quantise_weight(key, grouped):
+            codes = w_q_pool.tile([P, PASSES * BLOCK], U32, tag="w_codes", align_bytes=64, name="codes_w")
+            scales = w_q_pool.tile([P, PASSES * BLOCK], U8, tag="w_scales", align_bytes=64, name="scales_w")
+            nc.vector.quantize_mx(out=codes[:].bitcast(FP8X4), scales=scales[:], in_=grouped[:])
+            w_q[key] = (codes, scales)
+
+        x_grouped, x_view = new_grouped_rows("grouped_x")
+        x_flipped = flip(x_sb[:])
+        for g in range(PASSES):
+            copy = nc.scalar.copy if g % 2 == 0 else nc.vector.tensor_copy
+            copy(out=x_view[:, g], in_=x_flipped[:, g].unsqueeze(1).to_broadcast([P, GROUP_SLOTS, P, PACK]))
+        h0_grouped = group_rows("h", 0)
+        quantise_rows(("x", 0), x_grouped)
+        first_grouped = [(name, group_weight(name, 0, nc.vector.tensor_copy)) for name in PHASE_WEIGHTS["o"]]
+        quantise_rows(("h", 0), h0_grouped)
+        for name, grouped in first_grouped:
+            quantise_weight((name, 0), grouped)
+
+        def add_passes(acc, weight_q, u, moving_q, first, last):
+            w_codes, w_scales = weight_q
+            r_codes, r_scales = moving_q
+            for g in range(PASSES):
+                m_cols = slice(g * BLOCK + u * P, g * BLOCK + (u + 1) * P)
+                n_cols = slice(g * ROWS, (g + 1) * ROWS)
+                nc.tensor.matmul_mx(
+                    out=acc[:],
+                    lhsT=w_codes[:, m_cols].bitcast(FP8X4),
+                    lhsT_scale=w_scales[:, m_cols],
+                    rhs=r_codes[:, n_cols].bitcast(FP8X4),
+                    rhs_scale=r_scales[:, n_cols],
+                    start=(first and g == 0),
+                    stop=(last and g == PASSES - 1),
+                )
+
+        def multiply(step):
+            kind, jp, r = step
+            names = PHASE_WEIGHTS[kind]
+            banks = {}
+            for u in range(UNITS):
+                acc = acc_pool.tile([P, ROWS], F32, tag="acc", name="acc_gate")
+                add_passes(acc, w_q[(names[0], jp)], u, rows_q[("h", r)], True, False)
+                add_passes(acc, w_q[(names[1], jp)], u, rows_q[("x", 0)], False, True)
+                banks[("gate", u)] = acc
+            if kind == "ig":
+                for u in range(UNITS):
+                    acc = acc_pool.tile([P, ROWS], F32, tag="acc", name="acc_prop")
+                    add_passes(acc, w_q[("g", jp)], u, rows_q[("p", r)], True, True)
+                    banks[("prop", u)] = acc
+            return banks
+
+        def activate(step, banks):
+            kind, jp, r = step
+            tiles = {}
+            gate = work.tile([P, UNITS, ROWS], F32, tag="gate", name="gate")
+            for u in range(UNITS):
+                nc.scalar.activation(
+                    out=gate[:, u, :], in_=banks[("gate", u)][:], func=ACT.Sigmoid, bias=bias_col(kind[0], jp, u)
+                )
+            if kind != "f":
+                nc.scalar.activation(out=gate[:], in_=gate[:], func=ACT.Sigmoid)
+            tiles["gate"] = gate
+            if kind == "o":
+                tanh_m = work.tile([P, GROUP_SLOTS, BLOCK], F32, tag="tanh", bufs=2, name="tanh_m")
+                nc.scalar.activation(
+                    out=tanh_m[:], in_=m_blocks[jp][:, r * GROUP_SLOTS : (r + 1) * GROUP_SLOTS, :], func=ACT.Tanh
+                )
+                tiles["tanh"] = tanh_m
+            if kind == "ig":
+                prop = work.tile([P, UNITS, ROWS], F32, tag="prop", bufs=2, name="prop")
+                p_view = p_grouped[r][:].rearrange("c (g w t) -> c g w t", g=PASSES, w=ROWS, t=PACK)
+                for u in range(UNITS):
+                    j = jp * UNITS + u
+                    nc.vector.scalar_tensor_tensor(
+                        out=prop[:, u, :],
+                        in0=banks[("prop", u)][:],
+                        scalar=bias_col("g", jp, u),
+                        in1=p_view[:, j // PACK, :, j % PACK],
+                        op0=ALU.add,
+                        op1=ALU.add,
+                    )
+                tiles["prop"] = prop
+            return tiles
+
+        def flip_back(step, tiles):
+            kind = step[0]
+            result = tiles["gate"]
+            if kind == "ig":
+                result = tiles["prop"]
+                nc.vector.tensor_tensor(out=result[:], in0=result[:], in1=tiles["gate"][:], op=ALU.mult)
+            for u in range(UNITS):
+                back = back_pool.tile([P, GROUP_SLOTS, P], F32, tag="back", name="back")
+                for s in range(GROUP_SLOTS):
+                    nc.tensor.transpose(back[:, s, :], result[:, u, s * P : (s + 1) * P], ident_f[:])
+                tiles[("back", u)] = back
+
+        kept = {}
+
+        def finish(step, tiles):
+            kind, jp, r = step
+            slots = slice(r * GROUP_SLOTS, (r + 1) * GROUP_SLOTS)
+            features = slice(jp * BLOCK, (jp + 1) * BLOCK)
+            if kind == "ig":
+                out_tile = kept[(jp, r)]
+            else:
+                out_tile = work.tile([P, GROUP_SLOTS, BLOCK], F32, tag="out_" + kind, bufs=OUT_BUFS[kind], name="out_" + kind)
+            for u in range(UNITS):
+                cols = slice(u * P, (u + 1) * P)
+                other = {"o": tiles.get("tanh"), "f": m_blocks[jp][:, slots, :], "ig": out_tile}[kind]
+                nc.vector.tensor_tensor(
+                    out=out_tile[:, :, cols],
+                    in0=tiles[("back", u)][:],
+                    in1=other[:, :, cols],
+                    op=(ALU.add if kind == "ig" else ALU.mult),
+                )
+            if kind == "f":
+                nc.scalar.activation(out=out_tile[:], in_=out_tile[:], func=ACT.Sigmoid, bias=1.0)
+                kept[(jp, r)] = out_tile
+            if kind == "o":
+                nc.gpsimd.dma_start(out=out_1[:, slots, features], in_=out_tile[:])
+            if kind == "ig":
+                nc.gpsimd.dma_start(out=out_0[:, slots, features], in_=out_tile[:])
+
+        def prepare(f, r, copy):
+            if f >= len(phases):
+                return []
+            kind, jp = phases[f]
+            names = PHASE_WEIGHTS[kind]
+            half = (len(names) + 1) // 2
+            mine = names[:half] if r == 0 else names[half:]
+            made = [("w", (name, jp), group_weight(name, jp, copy)) for name in mine]
+            if (kind, jp) == ("ig", 0):
+                p_grouped[r] = group_rows("p", r)
+                made.append(("rows", ("p", r), p_grouped[r]))
+            return made
+
+        def quantise(made):
+            for what, key, grouped in made:
+                if what == "w":
+                    quantise_weight(key, grouped)
+                else:
+                    quantise_rows(key, grouped)
+
+        banks = multiply(steps[0])
+        quantise([("rows", ("h", 1), group_rows("h", 1))])
+        quantise(prepare(1, 0, nc.vector.tensor_copy) + prepare(1, 1, nc.scalar.copy))
+        waiting = []
+        tiles_of = {}
+        for i, step in enumerate(steps):
+            tiles_of[i] = activate(step, banks)
+            if i + 1 < len(steps):
+                banks = multiply(steps[i + 1])
+            if i >= 1:
+                finish(steps[i - 1], tiles_of[i - 1])
+            flip_back(step, tiles_of[i])
+            quantise(waiting)
+            copy = nc.scalar.copy if step[0] == "ig" else nc.vector.tensor_copy
+            waiting = prepare(i // ROW_GROUPS + 2, i % ROW_GROUPS, copy)
+        finish(steps[-1], tiles_of[len(steps) - 1])

@@ -61,7 +61,6 @@ def tile_relationalmemorycorecell_pa_kernel(
         make_identity(nc, ident_f[:])
         ident_b = const.tile([P, P], BF16, name="ident_b")
         make_identity(nc, ident_b[:])
-        ctx.enter_context(tc.manual_schedule())
 
         x_sb = const.tile([P, WIDTH], BF16, name="x_sb")
         rows_raw = {}

@@ -6,6 +6,7 @@ from concourse.masks import make_identity
 F32 = mybir.dt.float32
 BF16 = mybir.dt.bfloat16
 U32 = mybir.dt.uint32
+I32 = mybir.dt.int32
 U8 = mybir.dt.uint8
 FP8X4 = mybir.dt.float8_e4m3fn_x4
 ACT = mybir.ActivationFunctionType
@@ -18,6 +19,7 @@ PACK = 4
 PASSES = WIDTH // (P * PACK)
 K_TILES = WIDTH // P
 GROUP_SLOTS = 4
+SLOT_PAIR = 2
 ROWS = GROUP_SLOTS * P
 ROW_GROUPS = SLOTS // GROUP_SLOTS
 UNITS = 2
@@ -29,6 +31,9 @@ FLOPS = 2 * P * SLOTS * WIDTH * WIDTH * 4 + 2 * P * WIDTH * WIDTH * 3
 PHASE_WEIGHTS = {"o": ("uo", "wo"), "f": ("uf", "wf"), "ig": ("ui", "wi", "g")}
 BIAS_ORDER = ("g", "f", "i", "o")
 OUT_BUFS = {"o": 3, "f": 7}
+PHASES = [("o", 0), ("f", 0), ("o", 1), ("f", 1), ("o", 2), ("ig", 0), ("f", 2), ("ig", 1), ("o", 3), ("ig", 2), ("f", 3), ("ig", 3)]
+SHARES = {"o": ((3, 0), (3, 0)), "f": ((2, 2), (3, 1)), "ig": ((0, 1), (0, 1))}
+PINNED = {mybir.EngineType.PE, mybir.EngineType.DVE, mybir.EngineType.Activation}
 
 
 def tile_relationalmemorycorecell_pa_kernel(
@@ -39,12 +44,7 @@ def tile_relationalmemorycorecell_pa_kernel(
     bias_of = {"g": b_g, "f": b_uf, "i": b_ui, "o": b_uo}
     rows_of = {"h": h_state, "p": mem_att}
 
-    phases = []
-    for jp in range(BLOCKS + 1):
-        if jp < BLOCKS:
-            phases.extend([("o", jp), ("f", jp)])
-        if jp >= 1:
-            phases.append(("ig", jp - 1))
+    phases = PHASES
     steps = [(kind, jp, r) for (kind, jp) in phases for r in range(ROW_GROUPS)]
 
     with ExitStack() as ctx:
@@ -59,8 +59,6 @@ def tile_relationalmemorycorecell_pa_kernel(
 
         ident_f = const.tile([P, P], F32, name="ident_f")
         make_identity(nc, ident_f[:])
-        ident_b = const.tile([P, P], BF16, name="ident_b")
-        make_identity(nc, ident_b[:])
 
         x_sb = const.tile([P, WIDTH], BF16, name="x_sb")
         rows_raw = {}
@@ -70,104 +68,107 @@ def tile_relationalmemorycorecell_pa_kernel(
         def load_rows(name, r):
             raw = rows_pool.tile([P, GROUP_SLOTS * WIDTH], BF16, tag="rows_raw", name="raw_" + name)
             src = rows_of[name][:, r * GROUP_SLOTS : (r + 1) * GROUP_SLOTS, :]
-            nc.sync.dma_start(out=raw[:], in_=src.rearrange("b s n -> b (s n)"))
+            if name == "h":
+                for s in range(GROUP_SLOTS):
+                    nc.sync.dma_start(out=raw[:, s * WIDTH : (s + 1) * WIDTH], in_=src[:, s, :])
+            else:
+                nc.sync.dma_start(out=raw[:], in_=src.rearrange("b s n -> b (s n)"))
             rows_raw[(name, r)] = raw
 
         def load_weight(name, jp):
             raw = w_raw_pool.tile([P, K_TILES, BLOCK], BF16, tag="w_raw", name="raw_" + name)
             src = weight_of[name][:, jp * BLOCK : (jp + 1) * BLOCK]
-            nc.sync.dma_start(out=raw[:], in_=src.rearrange("(a c) n -> c a n", c=P))
+            dst_pairs = raw[:].rearrange("c (a e) n -> c a e n", e=2)
+            src_pairs = src.rearrange("(a c e) n -> c a e n", c=P, e=2)
+            for e in range(2):
+                nc.sync.dma_start(out=dst_pairs[:, :, e, :], in_=src_pairs[:, :, e, :])
             w_raw[(name, jp)] = raw
 
+        def load_m(jp):
+            m_block = const.tile([P, SLOTS, BLOCK], BF16, name="m_block%d" % jp)
+            nc.sync.dma_start(out=m_block[:], in_=m_state[:, :, jp * BLOCK : (jp + 1) * BLOCK])
+            m_blocks[jp] = m_block
+
         nc.sync.dma_start(out=x_sb[:], in_=inputs)
+        load_weight("wo", 0)
+        load_weight("uo", 0)
         load_rows("h", 0)
+        load_weight("uf", 0)
+        load_rows("h", 1)
         for kind, jp in phases:
             if (kind, jp) == ("ig", 0):
                 load_rows("p", 0)
                 load_rows("p", 1)
             for name in PHASE_WEIGHTS[kind]:
-                load_weight(name, jp)
-            if (kind, jp) == ("o", 0):
-                load_rows("h", 1)
-            if kind == "o":
-                m_block = const.tile([P, SLOTS, BLOCK], BF16, name="m_block%d" % jp)
-                nc.sync.dma_start(out=m_block[:], in_=m_state[:, :, jp * BLOCK : (jp + 1) * BLOCK])
-                m_blocks[jp] = m_block
+                if (name, jp) not in w_raw:
+                    load_weight(name, jp)
+            if (kind, jp) == phases[1]:
+                load_m(phases[0][1])
+            if kind == "o" and jp > 0:
+                load_m(jp)
 
-        bias_rows = const.tile([P, P], BF16, name="bias_rows")
+        bias_rows = const.tile([P, BLOCK], BF16, name="bias_rows")
         nc.vector.memset(bias_rows[:], 0.0)
         for k, key in enumerate(BIAS_ORDER):
             nc.scalar.dma_start(
-                out=bias_rows[k * K_TILES : (k + 1) * K_TILES, :],
-                in_=bias_of[key].rearrange("(j c) -> j c", c=P),
+                out=bias_rows[k * BLOCKS : (k + 1) * BLOCKS, :],
+                in_=bias_of[key].rearrange("(j n) -> j n", n=BLOCK),
             )
-        bias_flipped = back_pool.tile([P, WIDTH], BF16, tag="back", name="bias_flipped")
-        nc.tensor.transpose(bias_flipped[:, 0:P], bias_rows[:], ident_b[:])
         bias_cols = const.tile([P, P], F32, name="bias_cols")
-        nc.vector.tensor_copy(out=bias_cols[:], in_=bias_flipped[:, 0:P])
 
         def bias_col(key, jp, u):
-            col = BIAS_ORDER.index(key) * K_TILES + jp * UNITS + u
+            col = (BIAS_ORDER.index(key) * BLOCKS + jp) * UNITS + u
             return bias_cols[:, col : col + 1]
 
         rows_q = {}
         w_q = {}
-        p_grouped = {}
+        grouped_of = {}
 
-        def flip(raw_cols):
-            flipped = back_pool.tile([P, WIDTH], BF16, tag="back", name="flipped")
-            for a in range(K_TILES):
-                nc.tensor.transpose(flipped[:, a * P : (a + 1) * P], raw_cols[:, a * P : (a + 1) * P], ident_b[:])
-            return flipped[:].rearrange("c (g t b) -> c g b t", g=PASSES, t=PACK, b=P)
+        def flip_words(raw_cols):
+            flipped = back_pool.tile([P, WIDTH // 2], F32, tag="back", name="flipped_words")
+            words = raw_cols.bitcast(F32)
+            for a in range(WIDTH // 2 // P):
+                nc.tensor.transpose(flipped[:, a * P : (a + 1) * P], words[:, a * P : (a + 1) * P], ident_f[:])
+            return flipped[:].rearrange("c (g u b) -> c g b u", g=PASSES, u=2, b=P)
 
         def new_grouped_rows(name):
             grouped = rows_pool.tile([P, PASSES * ROWS * PACK], BF16, tag="rows_grouped", align_bytes=64, name=name)
-            view = grouped[:].rearrange("c (g s b t) -> c g s b t", g=PASSES, s=GROUP_SLOTS, b=P, t=PACK)
+            view = grouped[:].bitcast(F32).rearrange("c (g s b u) -> c g s b u", g=PASSES, s=GROUP_SLOTS, b=P, u=2)
             return grouped, view
 
-        def quantise_rows(key, grouped):
+        def quantise_rows(key):
+            grouped = grouped_of[key][0]
             codes = const.tile([P, PASSES * ROWS], U32, align_bytes=64, name="codes_%s%d" % key)
             scales = const.tile([P, PASSES * ROWS], U8, align_bytes=64, name="scales_%s%d" % key)
             nc.vector.quantize_mx(out=codes[:].bitcast(FP8X4), scales=scales[:], in_=grouped[:])
             rows_q[key] = (codes, scales)
 
-        def group_rows(name, r):
-            grouped, view = new_grouped_rows("grouped_" + name)
+        def group_slot(name, r, s, copy):
+            if (name, r) not in grouped_of:
+                grouped_of[(name, r)] = new_grouped_rows("grouped_" + name)
+            grouped, view = grouped_of[(name, r)]
             raw = rows_raw[(name, r)]
-            for s in range(GROUP_SLOTS):
-                flipped = flip(raw[:, s * WIDTH : (s + 1) * WIDTH])
-                copy = nc.scalar.copy if s % 2 == 0 else nc.vector.tensor_copy
-                copy(out=view[:, :, s, :, :], in_=flipped)
-            return grouped
+            flipped = flip_words(raw[:, s * WIDTH : (s + 1) * WIDTH])
+            copy(out=view[:, :, s, :, :], in_=flipped)
 
-        def group_weight(name, jp, copy):
+        def group_weight(name, jp, g, copy):
             raw = w_raw[(name, jp)]
-            grouped = w_grouped_pool.tile([P, PASSES * BLOCK * PACK], BF16, tag="w_grouped", align_bytes=64, name="grouped_w")
-            for g in range(PASSES):
-                dst = grouped[:, g * BLOCK * PACK : (g + 1) * BLOCK * PACK]
-                copy(
-                    out=dst.rearrange("c (n i t) -> c n t i", i=4, t=PACK),
-                    in_=raw[:, g * PACK : (g + 1) * PACK, :].rearrange("c t (n i) -> c n t i", i=4),
+            if (name, jp) not in grouped_of:
+                grouped_of[(name, jp)] = w_grouped_pool.tile(
+                    [P, PASSES * BLOCK * PACK], BF16, tag="w_grouped", align_bytes=64, name="grouped_w"
                 )
-            return grouped
+            dst = grouped_of[(name, jp)][:, g * BLOCK * PACK : (g + 1) * BLOCK * PACK]
+            copy(
+                out=dst.rearrange("c (u n i t) -> c n t i u", u=UNITS, i=2, t=PACK),
+                in_=raw[:, g * PACK : (g + 1) * PACK, :].rearrange("c t (n i u) -> c n t i u", u=UNITS, i=2),
+            )
 
-        def quantise_weight(key, grouped):
+        def quantise_weight(key):
+            grouped = grouped_of[key]
             codes = w_q_pool.tile([P, PASSES * BLOCK], U32, tag="w_codes", align_bytes=64, name="codes_w")
             scales = w_q_pool.tile([P, PASSES * BLOCK], U8, tag="w_scales", align_bytes=64, name="scales_w")
             nc.vector.quantize_mx(out=codes[:].bitcast(FP8X4), scales=scales[:], in_=grouped[:])
             w_q[key] = (codes, scales)
-
-        x_grouped, x_view = new_grouped_rows("grouped_x")
-        x_flipped = flip(x_sb[:])
-        for g in range(PASSES):
-            copy = nc.scalar.copy if g % 2 == 0 else nc.vector.tensor_copy
-            copy(out=x_view[:, g], in_=x_flipped[:, g].unsqueeze(1).to_broadcast([P, GROUP_SLOTS, P, PACK]))
-        h0_grouped = group_rows("h", 0)
-        quantise_rows(("x", 0), x_grouped)
-        first_grouped = [(name, group_weight(name, 0, nc.vector.tensor_copy)) for name in PHASE_WEIGHTS["o"]]
-        quantise_rows(("h", 0), h0_grouped)
-        for name, grouped in first_grouped:
-            quantise_weight((name, 0), grouped)
 
         def add_passes(acc, weight_q, u, moving_q, first, last):
             w_codes, w_scales = weight_q
@@ -185,20 +186,29 @@ def tile_relationalmemorycorecell_pa_kernel(
                     stop=(last and g == PASSES - 1),
                 )
 
-        def multiply(step):
+        def multiply_inputs(step):
             kind, jp, r = step
-            names = PHASE_WEIGHTS[kind]
             banks = {}
             for u in range(UNITS):
                 acc = acc_pool.tile([P, ROWS], F32, tag="acc", name="acc_gate")
-                add_passes(acc, w_q[(names[0], jp)], u, rows_q[("h", r)], True, False)
-                add_passes(acc, w_q[(names[1], jp)], u, rows_q[("x", 0)], False, True)
+                add_passes(acc, w_q[(PHASE_WEIGHTS[kind][1], jp)], u, rows_q[("x", 0)], True, False)
                 banks[("gate", u)] = acc
+            return banks
+
+        def multiply_rows(step, banks):
+            kind, jp, r = step
+            names = PHASE_WEIGHTS[kind]
+            for u in range(UNITS):
+                add_passes(banks[("gate", u)], w_q[(names[0], jp)], u, rows_q[("h", r)], False, True)
             if kind == "ig":
                 for u in range(UNITS):
                     acc = acc_pool.tile([P, ROWS], F32, tag="acc", name="acc_prop")
                     add_passes(acc, w_q[("g", jp)], u, rows_q[("p", r)], True, True)
                     banks[("prop", u)] = acc
+
+        def multiply(step):
+            banks = multiply_inputs(step)
+            multiply_rows(step, banks)
             return banks
 
         def activate(step, banks):
@@ -220,31 +230,33 @@ def tile_relationalmemorycorecell_pa_kernel(
                 tiles["tanh"] = tanh_m
             if kind == "ig":
                 prop = work.tile([P, UNITS, ROWS], F32, tag="prop", bufs=2, name="prop")
-                p_view = p_grouped[r][:].rearrange("c (g w t) -> c g w t", g=PASSES, w=ROWS, t=PACK)
+                p_view = grouped_of[("p", r)][0][:].rearrange("c (g w t) -> c g w t", g=PASSES, w=ROWS, t=PACK)
                 for u in range(UNITS):
-                    j = jp * UNITS + u
                     nc.vector.scalar_tensor_tensor(
                         out=prop[:, u, :],
                         in0=banks[("prop", u)][:],
                         scalar=bias_col("g", jp, u),
-                        in1=p_view[:, j // PACK, :, j % PACK],
+                        in1=p_view[:, jp // UNITS, :, jp % UNITS * UNITS + u],
                         op0=ALU.add,
                         op1=ALU.add,
                     )
                 tiles["prop"] = prop
             return tiles
 
+        def weigh(step, tiles):
+            if step[0] == "ig":
+                prop = tiles["prop"]
+                nc.vector.tensor_tensor(out=prop[:], in0=prop[:], in1=tiles["gate"][:], op=ALU.mult)
+
         def flip_back(step, tiles):
-            kind = step[0]
-            result = tiles["gate"]
-            if kind == "ig":
-                result = tiles["prop"]
-                nc.vector.tensor_tensor(out=result[:], in0=result[:], in1=tiles["gate"][:], op=ALU.mult)
-            for u in range(UNITS):
-                back = back_pool.tile([P, GROUP_SLOTS, P], F32, tag="back", name="back")
-                for s in range(GROUP_SLOTS):
-                    nc.tensor.transpose(back[:, s, :], result[:, u, s * P : (s + 1) * P], ident_f[:])
-                tiles[("back", u)] = back
+            result = tiles["prop" if step[0] == "ig" else "gate"]
+            for v in range(UNITS):
+                back = back_pool.tile([P, SLOT_PAIR, UNITS, P], F32, tag="back", name="back")
+                for s in range(SLOT_PAIR):
+                    rows = slice((SLOT_PAIR * v + s) * P, (SLOT_PAIR * v + s + 1) * P)
+                    for u in range(UNITS):
+                        nc.tensor.transpose(back[:, s, u, :], result[:, u, rows], ident_f[:])
+                tiles[("back", v)] = back
 
         kept = {}
 
@@ -256,13 +268,13 @@ def tile_relationalmemorycorecell_pa_kernel(
                 out_tile = kept[(jp, r)]
             else:
                 out_tile = work.tile([P, GROUP_SLOTS, BLOCK], F32, tag="out_" + kind, bufs=OUT_BUFS[kind], name="out_" + kind)
-            for u in range(UNITS):
-                cols = slice(u * P, (u + 1) * P)
+            for v in range(UNITS):
+                pair = slice(v * SLOT_PAIR, (v + 1) * SLOT_PAIR)
                 other = {"o": tiles.get("tanh"), "f": m_blocks[jp][:, slots, :], "ig": out_tile}[kind]
                 nc.vector.tensor_tensor(
-                    out=out_tile[:, :, cols],
-                    in0=tiles[("back", u)][:],
-                    in1=other[:, :, cols],
+                    out=out_tile[:, pair, :].rearrange("b s (c u) -> b s c u", u=UNITS),
+                    in0=tiles[("back", v)][:].rearrange("b s u c -> b s c u"),
+                    in1=other[:, pair, :].rearrange("b s (c u) -> b s c u", u=UNITS),
                     op=(ALU.add if kind == "ig" else ALU.mult),
                 )
             if kind == "f":
@@ -273,39 +285,109 @@ def tile_relationalmemorycorecell_pa_kernel(
             if kind == "ig":
                 nc.gpsimd.dma_start(out=out_0[:, slots, features], in_=out_tile[:])
 
-        def prepare(f, r, copy):
-            if f >= len(phases):
-                return []
-            kind, jp = phases[f]
-            names = PHASE_WEIGHTS[kind]
-            half = (len(names) + 1) // 2
-            mine = names[:half] if r == 0 else names[half:]
-            made = [("w", (name, jp), group_weight(name, jp, copy)) for name in mine]
+        ctx.enter_context(tc.manual_schedule(engines=PINNED))
+        SC, VC = nc.scalar.copy, nc.vector.tensor_copy
+        H0 = [SC, SC, SC, SC]
+        H1 = [SC, VC, SC, VC]
+        WO = [VC, VC]
+        UO = [VC, SC]
+        UF = [(2, VC), (1, SC), (1, VC)]
+        x_grouped = const.tile([P, WIDTH], BF16, align_bytes=64, name="grouped_x")
+        nc.scalar.copy(
+            out=x_grouped[:].bitcast(F32).rearrange("c (g b u) -> c g b u", g=PASSES, b=P, u=2), in_=flip_words(x_sb[:])
+        )
+        bias_flipped = back_pool.tile([P, P], F32, tag="back", name="bias_flipped")
+        nc.tensor.transpose(bias_flipped[:], bias_rows[:].bitcast(F32), ident_f[:])
+        n_bias = len(BIAS_ORDER) * BLOCKS * UNITS
+        nc.vector.tensor_copy(out=bias_cols[:, 0:n_bias], in_=bias_flipped[:].bitcast(BF16)[:, 0:n_bias])
+        x_codes = const.tile([P, PASSES, P], U32, align_bytes=64, name="x_codes")
+        x_scales = const.tile([P, PASSES, P], U8, align_bytes=64, name="x_scales")
+        nc.gpsimd.memset(x_scales[:].rearrange("c g b -> c (g b)").bitcast(I32), 0)
+        nc.vector.quantize_mx(
+            out=x_codes[:].rearrange("c g b -> c (g b)").bitcast(FP8X4),
+            scales=x_scales[:].rearrange("c g b -> c (g b)"),
+            in_=x_grouped[:],
+        )
+        codes_x = const.tile([P, PASSES * ROWS], U32, align_bytes=64, name="codes_x")
+        scales_x = const.tile([P, PASSES * ROWS], U8, align_bytes=64, name="scales_x")
+        for many, one, n in ((codes_x, x_codes, P), (scales_x, x_scales, P // 4)):
+            nc.vector.tensor_copy(
+                out=many[:].bitcast(I32).rearrange("c (g s n) -> c g s n", g=PASSES, s=GROUP_SLOTS, n=n),
+                in_=one[:].bitcast(I32).unsqueeze(2).to_broadcast([P, PASSES, GROUP_SLOTS, n]),
+            )
+        rows_q[("x", 0)] = (codes_x, scales_x)
+        for g in range(PASSES):
+            group_weight("wo", 0, g, WO[g])
+        quantise_weight(("wo", 0))
+        for g in range(PASSES):
+            group_weight("uo", 0, g, UO[g])
+        for s in range(GROUP_SLOTS):
+            group_slot("h", 0, s, H0[s])
+        banks = multiply_inputs(steps[0])
+        quantise_weight(("uo", 0))
+        quantise_rows(("h", 0))
+        tasks = []
+        for kind, jp in phases:
             if (kind, jp) == ("ig", 0):
-                p_grouped[r] = group_rows("p", r)
-                made.append(("rows", ("p", r), p_grouped[r]))
-            return made
-
-        def quantise(made):
-            for what, key, grouped in made:
-                if what == "w":
-                    quantise_weight(key, grouped)
-                else:
-                    quantise_rows(key, grouped)
-
-        banks = multiply(steps[0])
-        quantise([("rows", ("h", 1), group_rows("h", 1))])
-        quantise(prepare(1, 0, nc.vector.tensor_copy) + prepare(1, 1, nc.scalar.copy))
+                for r in range(ROW_GROUPS):
+                    tasks.extend([("slot", ("p", r), s) for s in range(GROUP_SLOTS)])
+            for name in PHASE_WEIGHTS[kind]:
+                if (kind, jp) != ("o", 0):
+                    tasks.extend([("half", (name, jp), g) for g in range(PASSES)])
         waiting = []
+
+        def run_tasks(count, weight_copy, slot_copy):
+            for what, key, part in tasks[:count]:
+                if what == "half":
+                    group_weight(key[0], key[1], part, weight_copy)
+                    if part == PASSES - 1:
+                        waiting.append((what, key))
+                else:
+                    group_slot(key[0], key[1], part, slot_copy)
+                    if part == GROUP_SLOTS - 1:
+                        waiting.append((what, key))
+            for task in tasks[:count]:
+                tasks.remove(task)
+
+        def run_quantises():
+            for what, key in waiting:
+                if what == "half":
+                    quantise_weight(key)
+                else:
+                    quantise_rows(key)
+            waiting.clear()
+
+        def ensure(step):
+            kind, jp, r = step
+            keys = [(n, jp) for n in PHASE_WEIGHTS[kind]]
+            while any([k not in w_q for k in keys]) or (kind == "ig" and ("p", r) not in rows_q):
+                if not waiting:
+                    run_tasks(1, nc.vector.tensor_copy, nc.scalar.copy)
+                run_quantises()
+
+        for count, copy in UF[0:1]:
+            run_tasks(count, copy, copy)
+        run_quantises()
+        multiply_rows(steps[0], banks)
+        for s in range(GROUP_SLOTS):
+            group_slot("h", 1, s, H1[s])
+        quantise_rows(("h", 1))
+        for count, copy in UF[1:]:
+            run_tasks(count, copy, copy)
         tiles_of = {}
         for i, step in enumerate(steps):
             tiles_of[i] = activate(step, banks)
+            if i >= 1:
+                flip_back(steps[i - 1], tiles_of[i - 1])
             if i + 1 < len(steps):
+                ensure(steps[i + 1])
                 banks = multiply(steps[i + 1])
             if i >= 1:
                 finish(steps[i - 1], tiles_of[i - 1])
-            flip_back(step, tiles_of[i])
-            quantise(waiting)
-            copy = nc.scalar.copy if step[0] == "ig" else nc.vector.tensor_copy
-            waiting = prepare(i // ROW_GROUPS + 2, i % ROW_GROUPS, copy)
+            run_quantises()
+            for_vector, for_scalar = SHARES[step[0]][step[2]]
+            run_tasks(for_vector, nc.vector.tensor_copy, nc.vector.tensor_copy)
+            run_tasks(for_scalar, nc.scalar.copy, nc.scalar.copy)
+            weigh(step, tiles_of[i])
+        flip_back(steps[-1], tiles_of[len(steps) - 1])
         finish(steps[-1], tiles_of[len(steps) - 1])

@@ -25,13 +25,15 @@ ROW_GROUPS = SLOTS // GROUP_SLOTS
 UNITS = 2
 BLOCK = UNITS * P
 BLOCKS = WIDTH // BLOCK
+LOAD = 2 * BLOCK
 
 FLOPS = 2 * P * SLOTS * WIDTH * WIDTH * 4 + 2 * P * WIDTH * WIDTH * 3
 
 PHASE_WEIGHTS = {"o": ("uo", "wo"), "f": ("uf", "wf"), "ig": ("ui", "wi", "g")}
 BIAS_ORDER = ("g", "f", "i", "o")
 OUT_BUFS = {"o": 3, "f": 7}
-PHASES = [("o", 0), ("f", 0), ("o", 1), ("f", 1), ("o", 2), ("ig", 0), ("f", 2), ("ig", 1), ("o", 3), ("ig", 2), ("f", 3), ("ig", 3)]
+W_RAW_BUFS = 5
+PHASES = [("o", 0), ("o", 1), ("f", 0), ("f", 1), ("o", 2), ("ig", 0), ("o", 3), ("ig", 1), ("f", 2), ("f", 3), ("ig", 2), ("ig", 3)]
 SHARES = {"o": ((3, 0), (3, 0)), "f": ((2, 2), (3, 1)), "ig": ((0, 1), (0, 1))}
 PINNED = {mybir.EngineType.PE, mybir.EngineType.DVE, mybir.EngineType.Activation}
 
@@ -50,7 +52,7 @@ def tile_relationalmemorycorecell_pa_kernel(
     with ExitStack() as ctx:
         const = ctx.enter_context(tc.tile_pool(name="const", bufs=1))
         rows_pool = ctx.enter_context(tc.tile_pool(name="rows", bufs=2))
-        w_raw_pool = ctx.enter_context(tc.tile_pool(name="w_raw", bufs=8))
+        w_raw_pool = ctx.enter_context(tc.tile_pool(name="w_raw", bufs=W_RAW_BUFS))
         w_grouped_pool = ctx.enter_context(tc.tile_pool(name="w_grouped", bufs=4))
         w_q_pool = ctx.enter_context(tc.tile_pool(name="w_q", bufs=9))
         work = ctx.enter_context(tc.tile_pool(name="work", bufs=3))
@@ -75,37 +77,50 @@ def tile_relationalmemorycorecell_pa_kernel(
                 nc.sync.dma_start(out=raw[:], in_=src.rearrange("b s n -> b (s n)"))
             rows_raw[(name, r)] = raw
 
-        def load_weight(name, jp):
-            raw = w_raw_pool.tile([P, K_TILES, BLOCK], BF16, tag="w_raw", name="raw_" + name)
-            src = weight_of[name][:, jp * BLOCK : (jp + 1) * BLOCK]
+        def load_weight(name, k):
+            raw = w_raw_pool.tile([P, K_TILES, LOAD], BF16, tag="w_raw", name="raw_" + name)
+            src = weight_of[name][:, k * LOAD : (k + 1) * LOAD]
             dst_pairs = raw[:].rearrange("c (a e) n -> c a e n", e=2)
             src_pairs = src.rearrange("(a c e) n -> c a e n", c=P, e=2)
             for e in range(2):
                 nc.sync.dma_start(out=dst_pairs[:, :, e, :], in_=src_pairs[:, :, e, :])
-            w_raw[(name, jp)] = raw
+            w_raw[(name, k)] = raw
 
-        def load_m(jp):
-            m_block = const.tile([P, SLOTS, BLOCK], BF16, name="m_block%d" % jp)
-            nc.sync.dma_start(out=m_block[:], in_=m_state[:, :, jp * BLOCK : (jp + 1) * BLOCK])
-            m_blocks[jp] = m_block
+        def load_m(k):
+            m_block = const.tile([P, SLOTS, LOAD], BF16, name="m_block%d" % k)
+            nc.sync.dma_start(out=m_block[:], in_=m_state[:, :, k * LOAD : (k + 1) * LOAD])
+            m_blocks[2 * k] = m_block[:, :, 0:BLOCK]
+            m_blocks[2 * k + 1] = m_block[:, :, BLOCK:LOAD]
 
-        nc.sync.dma_start(out=x_sb[:], in_=inputs)
-        load_weight("wo", 0)
-        load_weight("uo", 0)
-        load_rows("h", 0)
-        load_weight("uf", 0)
-        load_rows("h", 1)
+        to_load = [("x", 0), ("wo", 0), ("uo", 0), ("h", 0), ("uf", 0), ("h", 1), ("wf", 0), ("m", 0)]
         for kind, jp in phases:
             if (kind, jp) == ("ig", 0):
-                load_rows("p", 0)
-                load_rows("p", 1)
-            for name in PHASE_WEIGHTS[kind]:
-                if (name, jp) not in w_raw:
-                    load_weight(name, jp)
-            if (kind, jp) == phases[1]:
-                load_m(phases[0][1])
-            if kind == "o" and jp > 0:
-                load_m(jp)
+                to_load.extend([("p", 0), ("p", 1)])
+            for name in PHASE_WEIGHTS[kind] + (("m",) if kind == "o" else ()):
+                if (name, jp // 2) not in to_load:
+                    to_load.append((name, jp // 2))
+
+        def load_next_weight():
+            seen = False
+            while to_load and not (seen and to_load[0][0] in weight_of):
+                name, k = to_load.pop(0)
+                if name in weight_of:
+                    load_weight(name, k)
+                    seen = True
+                else:
+                    load_other((name, k))
+
+        def load_other(key):
+            name, k = key
+            if name == "x":
+                nc.sync.dma_start(out=x_sb[:], in_=inputs)
+            elif name == "m":
+                load_m(k)
+            else:
+                load_rows(name, k)
+
+        for count in range(W_RAW_BUFS):
+            load_next_weight()
 
         bias_rows = const.tile([P, BLOCK], BF16, name="bias_rows")
         nc.vector.memset(bias_rows[:], 0.0)
@@ -152,7 +167,7 @@ def tile_relationalmemorycorecell_pa_kernel(
             copy(out=view[:, :, s, :, :], in_=flipped)
 
         def group_weight(name, jp, g, copy):
-            raw = w_raw[(name, jp)]
+            raw = w_raw[(name, jp // 2)]
             if (name, jp) not in grouped_of:
                 grouped_of[(name, jp)] = w_grouped_pool.tile(
                     [P, PASSES * BLOCK * PACK], BF16, tag="w_grouped", align_bytes=64, name="grouped_w"
@@ -160,7 +175,9 @@ def tile_relationalmemorycorecell_pa_kernel(
             dst = grouped_of[(name, jp)][:, g * BLOCK * PACK : (g + 1) * BLOCK * PACK]
             copy(
                 out=dst.rearrange("c (u n i t) -> c n t i u", u=UNITS, i=2, t=PACK),
-                in_=raw[:, g * PACK : (g + 1) * PACK, :].rearrange("c t (n i u) -> c n t i u", u=UNITS, i=2),
+                in_=raw[:, g * PACK : (g + 1) * PACK, jp % 2 * BLOCK : (jp % 2 + 1) * BLOCK].rearrange(
+                    "c t (n i u) -> c n t i u", u=UNITS, i=2
+                ),
             )
 
         def quantise_weight(key):
@@ -280,10 +297,16 @@ def tile_relationalmemorycorecell_pa_kernel(
             if kind == "f":
                 nc.scalar.activation(out=out_tile[:], in_=out_tile[:], func=ACT.Sigmoid, bias=1.0)
                 kept[(jp, r)] = out_tile
+            tiles["out"] = out_tile
+
+        def store(step, tiles):
+            kind, jp, r = step
+            slots = slice(r * GROUP_SLOTS, (r + 1) * GROUP_SLOTS)
+            features = slice(jp * BLOCK, (jp + 1) * BLOCK)
             if kind == "o":
-                nc.gpsimd.dma_start(out=out_1[:, slots, features], in_=out_tile[:])
+                nc.scalar.dma_start(out=out_1[:, slots, features], in_=tiles["out"][:])
             if kind == "ig":
-                nc.gpsimd.dma_start(out=out_0[:, slots, features], in_=out_tile[:])
+                nc.scalar.dma_start(out=out_0[:, slots, features], in_=tiles["out"][:])
 
         ctx.enter_context(tc.manual_schedule(engines=PINNED))
         SC, VC = nc.scalar.copy, nc.vector.tensor_copy
@@ -342,6 +365,8 @@ def tile_relationalmemorycorecell_pa_kernel(
                     group_weight(key[0], key[1], part, weight_copy)
                     if part == PASSES - 1:
                         waiting.append((what, key))
+                        if key[1] % 2 == 1:
+                            load_next_weight()
                 else:
                     group_slot(key[0], key[1], part, slot_copy)
                     if part == GROUP_SLOTS - 1:
@@ -356,6 +381,9 @@ def tile_relationalmemorycorecell_pa_kernel(
                 else:
                     quantise_rows(key)
             waiting.clear()
+
+        def gpsimd_copy(out, in_):
+            nc.gpsimd.tensor_scalar(out=out, in0=in_, scalar1=1.0, scalar2=0.0, op0=ALU.mult, op1=ALU.add)
 
         def ensure(step):
             kind, jp, r = step
@@ -385,9 +413,13 @@ def tile_relationalmemorycorecell_pa_kernel(
             if i >= 1:
                 finish(steps[i - 1], tiles_of[i - 1])
             run_quantises()
-            for_vector, for_scalar = SHARES[step[0]][step[2]]
+            for_vector, for_scalar, for_gpsimd = (SHARES[step[0]][step[2]] + (0,))[:3]
             run_tasks(for_vector, nc.vector.tensor_copy, nc.vector.tensor_copy)
             run_tasks(for_scalar, nc.scalar.copy, nc.scalar.copy)
+            run_tasks(for_gpsimd, gpsimd_copy, nc.vector.tensor_copy)
+            if i >= 1:
+                store(steps[i - 1], tiles_of[i - 1])
             weigh(step, tiles_of[i])
         flip_back(steps[-1], tiles_of[len(steps) - 1])
         finish(steps[-1], tiles_of[len(steps) - 1])
+        store(steps[-1], tiles_of[len(steps) - 1])

@@ -17,7 +17,6 @@ SLOTS = 8
 WIDTH = 1024
 PACK = 4
 PASSES = WIDTH // (P * PACK)
-K_TILES = WIDTH // P
 GROUP_SLOTS = 4
 SLOT_PAIR = 2
 ROWS = GROUP_SLOTS * P
@@ -25,16 +24,28 @@ ROW_GROUPS = SLOTS // GROUP_SLOTS
 UNITS = 2
 BLOCK = UNITS * P
 BLOCKS = WIDTH // BLOCK
-LOAD = 2 * BLOCK
+HALF = 2 * BLOCK
 
 FLOPS = 2 * P * SLOTS * WIDTH * WIDTH * 4 + 2 * P * WIDTH * WIDTH * 3
 
 PHASE_WEIGHTS = {"o": ("uo", "wo"), "f": ("uf", "wf"), "ig": ("ui", "wi", "g")}
 BIAS_ORDER = ("g", "f", "i", "o")
-OUT_BUFS = {"o": 3, "f": 7}
+PHASES = [("o", 0), ("o", 1), ("f", 0), ("f", 1), ("o", 2), ("o", 3), ("ig", 0), ("ig", 1), ("f", 2), ("f", 3), ("ig", 2), ("ig", 3)]
+LOADS = [("x", 0), ("wo", 0, 0, 512), ("uo", 0, 0, 512), ("h", 0), ("h", 1), ("m", 0, 0), ("m", 1, 0), ("uf", 0, 0, 512), ("wf", 0, 0, 512), ("uo", 1, 0, 512), ("wo", 1, 0, 512), ("m", 0, 1), ("m", 1, 1), ("p", 0), ("p", 1), ("ui", 0, 0, 512), ("wi", 0, 0, 512), ("g", 0, 0, 512), ("uf", 1, 0, 512), ("wf", 1, 0, 512), ("ui", 1, 0, 512), ("wi", 1, 0, 512), ("g", 1, 0, 512)]
+TASKS = [("w", "uo", 1, 0), ("w", "uo", 1, 1), ("w", "wo", 1, 0), ("w", "wo", 1, 1), ("w", "uf", 0, 0), ("w", "uf", 0, 1), ("w", "wf", 0, 0), ("w", "wf", 0, 1), ("w", "uf", 1, 0), ("w", "uf", 1, 1), ("w", "wf", 1, 0), ("w", "wf", 1, 1), ("w", "uo", 2, 0), ("w", "uo", 2, 1), ("w", "wo", 2, 0), ("w", "wo", 2, 1), ("w", "uo", 3, 0), ("w", "uo", 3, 1), ("w", "wo", 3, 0), ("w", "wo", 3, 1), ("slot", "p", 0, 0), ("slot", "p", 0, 1), ("slot", "p", 0, 2), ("slot", "p", 0, 3), ("slot", "p", 1, 0), ("slot", "p", 1, 1), ("slot", "p", 1, 2), ("slot", "p", 1, 3), ("w", "ui", 0, 0), ("w", "ui", 0, 1), ("w", "wi", 0, 0), ("w", "wi", 0, 1), ("w", "g", 0, 0), ("w", "g", 0, 1), ("w", "ui", 1, 0), ("w", "ui", 1, 1), ("w", "wi", 1, 0), ("w", "wi", 1, 1), ("w", "g", 1, 0), ("w", "g", 1, 1), ("w", "uf", 2, 0), ("w", "uf", 2, 1), ("w", "wf", 2, 0), ("w", "wf", 2, 1), ("w", "uf", 3, 0), ("w", "uf", 3, 1), ("w", "wf", 3, 0), ("w", "wf", 3, 1), ("w", "ui", 2, 0), ("w", "ui", 2, 1), ("w", "wi", 2, 0), ("w", "wi", 2, 1), ("w", "g", 2, 0), ("w", "g", 2, 1), ("w", "ui", 3, 0), ("w", "ui", 3, 1), ("w", "wi", 3, 0), ("w", "wi", 3, 1), ("w", "g", 3, 0), ("w", "g", 3, 1)]
+SHARES = {"o":["VVV"],"f":["VVSS","VVVS"],"ig":["S"]}
+HEAD = {"w":"VV","u":"VS","h0":"SSSS","h1":"SVSV","t0":"VV","t1":"","t2":"SV"}
 W_RAW_BUFS = 5
-PHASES = [("o", 0), ("o", 1), ("f", 0), ("f", 1), ("o", 2), ("ig", 0), ("o", 3), ("ig", 1), ("f", 2), ("f", 3), ("ig", 2), ("ig", 3)]
-SHARES = {"o": ((3, 0), (3, 0)), "f": ((2, 2), (3, 1)), "ig": ((0, 1), (0, 1))}
+SPLIT_LOADS = 0
+W_Q_BUFS = 9
+GROUPED_BUFS = 4
+OUT_BUFS = {"o":3,"f":7}
+ACC_BUFS = 4
+INTER_BUFS = 0
+TANH_EARLY = False
+FINISH_LATE = True
+MULT_FIRST = {"o": True, "f": True, "ig": False}
+TASKS_FIRST = {"o": True, "f": True, "ig": True}
 PINNED = {mybir.EngineType.PE, mybir.EngineType.DVE, mybir.EngineType.Activation}
 
 
@@ -45,27 +56,35 @@ def tile_relationalmemorycorecell_pa_kernel(
     weight_of = {"g": W_g, "wf": W_wf, "wi": W_wi, "wo": W_wo, "uf": W_uf, "ui": W_ui, "uo": W_uo}
     bias_of = {"g": b_g, "f": b_uf, "i": b_ui, "o": b_uo}
     rows_of = {"h": h_state, "p": mem_att}
+    steps = [(kind, jp, r) for (kind, jp) in PHASES for r in range(ROW_GROUPS)]
+    SC, VC = nc.scalar.copy, nc.vector.tensor_copy
 
-    phases = PHASES
-    steps = [(kind, jp, r) for (kind, jp) in phases for r in range(ROW_GROUPS)]
+    def gpsimd_copy(out, in_):
+        nc.gpsimd.tensor_scalar(out=out, in0=in_, scalar1=1.0, scalar2=0.0, op0=ALU.mult, op1=ALU.add)
+
+    COPY = {"S": SC, "V": VC, "G": gpsimd_copy, "P": SC}
 
     with ExitStack() as ctx:
         const = ctx.enter_context(tc.tile_pool(name="const", bufs=1))
         rows_pool = ctx.enter_context(tc.tile_pool(name="rows", bufs=2))
         w_raw_pool = ctx.enter_context(tc.tile_pool(name="w_raw", bufs=W_RAW_BUFS))
-        w_grouped_pool = ctx.enter_context(tc.tile_pool(name="w_grouped", bufs=4))
-        w_q_pool = ctx.enter_context(tc.tile_pool(name="w_q", bufs=9))
+        w_grouped_pool = ctx.enter_context(tc.tile_pool(name="w_grouped", bufs=GROUPED_BUFS))
+        w_q_pool = ctx.enter_context(tc.tile_pool(name="w_q", bufs=W_Q_BUFS))
         work = ctx.enter_context(tc.tile_pool(name="work", bufs=3))
-        acc_pool = ctx.enter_context(tc.psum_pool(name="acc", bufs=4))
-        back_pool = ctx.enter_context(tc.psum_pool(name="back", bufs=4))
+        acc_pool = ctx.enter_context(tc.psum_pool(name="acc", bufs=ACC_BUFS))
+        back_pool = ctx.enter_context(tc.psum_pool(name="back", bufs=8 - ACC_BUFS - INTER_BUFS))
+        inter_pool = ctx.enter_context(tc.psum_pool(name="inter", bufs=INTER_BUFS)) if INTER_BUFS > 0 else back_pool
 
         ident_f = const.tile([P, P], F32, name="ident_f")
         make_identity(nc, ident_f[:])
+        ident_b = const.tile([P, P], BF16, name="ident_b")
+        make_identity(nc, ident_b[:])
 
         x_sb = const.tile([P, WIDTH], BF16, name="x_sb")
         rows_raw = {}
+        m_rows = {}
         w_raw = {}
-        m_blocks = {}
+        readers_left = {}
 
         def load_rows(name, r):
             raw = rows_pool.tile([P, GROUP_SLOTS * WIDTH], BF16, tag="rows_raw", name="raw_" + name)
@@ -77,49 +96,43 @@ def tile_relationalmemorycorecell_pa_kernel(
                 nc.sync.dma_start(out=raw[:], in_=src.rearrange("b s n -> b (s n)"))
             rows_raw[(name, r)] = raw
 
-        def load_weight(name, k):
-            raw = w_raw_pool.tile([P, K_TILES, LOAD], BF16, tag="w_raw", name="raw_" + name)
-            src = weight_of[name][:, k * LOAD : (k + 1) * LOAD]
-            dst_pairs = raw[:].rearrange("c (a e) n -> c a e n", e=2)
-            src_pairs = src.rearrange("(a c e) n -> c a e n", c=P, e=2)
+        def load_m(r, half):
+            m_rows[(r, half)] = const.tile([P, GROUP_SLOTS, HALF], BF16, name="m_rows%d%d" % (r, half))
+            nc.sync.dma_start(
+                out=m_rows[(r, half)][:],
+                in_=m_state[:, r * GROUP_SLOTS : (r + 1) * GROUP_SLOTS, half * HALF : (half + 1) * HALF],
+            )
+
+        def m_block(jp, r):
+            return m_rows[(r, jp // 2)][:, :, jp % 2 * BLOCK : (jp % 2 + 1) * BLOCK]
+
+        def load_weight(name, k, first, last):
+            if (name, k) not in w_raw:
+                raw = w_raw_pool.tile([P, 2 * PACK * HALF], BF16, tag="w_raw", name="raw_" + name)
+                w_raw[(name, k)] = raw
+                readers_left[(name, k)] = 4
+            dst = w_raw[(name, k)][:].rearrange("c (a e n) -> c a e n", e=2, n=HALF)[:, :, :, first:last]
+            src = weight_of[name][:, k * HALF + first : k * HALF + last].rearrange("(a c e) n -> c a e n", c=P, e=2)
             for e in range(2):
-                nc.sync.dma_start(out=dst_pairs[:, :, e, :], in_=src_pairs[:, :, e, :])
-            w_raw[(name, k)] = raw
+                nc.sync.dma_start(out=dst[:, :, e, :], in_=src[:, :, e, :])
 
-        def load_m(k):
-            m_block = const.tile([P, SLOTS, LOAD], BF16, name="m_block%d" % k)
-            nc.sync.dma_start(out=m_block[:], in_=m_state[:, :, k * LOAD : (k + 1) * LOAD])
-            m_blocks[2 * k] = m_block[:, :, 0:BLOCK]
-            m_blocks[2 * k + 1] = m_block[:, :, BLOCK:LOAD]
-
-        to_load = [("x", 0), ("wo", 0), ("uo", 0), ("h", 0), ("uf", 0), ("h", 1), ("wf", 0), ("m", 0)]
-        for kind, jp in phases:
-            if (kind, jp) == ("ig", 0):
-                to_load.extend([("p", 0), ("p", 1)])
-            for name in PHASE_WEIGHTS[kind] + (("m",) if kind == "o" else ()):
-                if (name, jp // 2) not in to_load:
-                    to_load.append((name, jp // 2))
+        loads = list(LOADS)
 
         def load_next_weight():
             seen = False
-            while to_load and not (seen and to_load[0][0] in weight_of):
-                name, k = to_load.pop(0)
-                if name in weight_of:
-                    load_weight(name, k)
-                    seen = True
+            while loads and not (seen and loads[0][0] in weight_of):
+                load = loads.pop(0)
+                seen = seen or load[0] in weight_of
+                if load[0] in weight_of:
+                    load_weight(load[0], load[1], load[2], load[3])
+                elif load[0] == "m":
+                    load_m(load[1], load[2])
+                elif load[0] == "x":
+                    nc.sync.dma_start(out=x_sb[:], in_=inputs)
                 else:
-                    load_other((name, k))
+                    load_rows(load[0], load[1])
 
-        def load_other(key):
-            name, k = key
-            if name == "x":
-                nc.sync.dma_start(out=x_sb[:], in_=inputs)
-            elif name == "m":
-                load_m(k)
-            else:
-                load_rows(name, k)
-
-        for count in range(W_RAW_BUFS):
+        for count in range(W_RAW_BUFS + SPLIT_LOADS):
             load_next_weight()
 
         bias_rows = const.tile([P, BLOCK], BF16, name="bias_rows")
@@ -146,51 +159,70 @@ def tile_relationalmemorycorecell_pa_kernel(
                 nc.tensor.transpose(flipped[:, a * P : (a + 1) * P], words[:, a * P : (a + 1) * P], ident_f[:])
             return flipped[:].rearrange("c (g u b) -> c g b u", g=PASSES, u=2, b=P)
 
-        def new_grouped_rows(name):
-            grouped = rows_pool.tile([P, PASSES * ROWS * PACK], BF16, tag="rows_grouped", align_bytes=64, name=name)
-            view = grouped[:].bitcast(F32).rearrange("c (g s b u) -> c g s b u", g=PASSES, s=GROUP_SLOTS, b=P, u=2)
-            return grouped, view
-
-        def quantise_rows(key):
-            grouped = grouped_of[key][0]
-            codes = const.tile([P, PASSES * ROWS], U32, align_bytes=64, name="codes_%s%d" % key)
-            scales = const.tile([P, PASSES * ROWS], U8, align_bytes=64, name="scales_%s%d" % key)
-            nc.vector.quantize_mx(out=codes[:].bitcast(FP8X4), scales=scales[:], in_=grouped[:])
-            rows_q[key] = (codes, scales)
-
         def group_slot(name, r, s, copy):
             if (name, r) not in grouped_of:
-                grouped_of[(name, r)] = new_grouped_rows("grouped_" + name)
-            grouped, view = grouped_of[(name, r)]
-            raw = rows_raw[(name, r)]
-            flipped = flip_words(raw[:, s * WIDTH : (s + 1) * WIDTH])
-            copy(out=view[:, :, s, :, :], in_=flipped)
+                grouped_of[(name, r)] = rows_pool.tile(
+                    [P, PASSES * ROWS * PACK], BF16, tag="rows_grouped", align_bytes=64, name="grouped_" + name
+                )
+            view = grouped_of[(name, r)][:].bitcast(F32).rearrange(
+                "c (g s b u) -> c g s b u", g=PASSES, s=GROUP_SLOTS, b=P, u=2
+            )
+            copy(out=view[:, :, s, :, :], in_=flip_words(rows_raw[(name, r)][:, s * WIDTH : (s + 1) * WIDTH]))
+
+        def quantise_rows(key):
+            codes = const.tile([P, PASSES * ROWS], U32, align_bytes=64, name="codes_%s%d" % key)
+            scales = const.tile([P, PASSES * ROWS], U8, align_bytes=64, name="scales_%s%d" % key)
+            nc.vector.quantize_mx(out=codes[:].bitcast(FP8X4), scales=scales[:], in_=grouped_of[key][:])
+            rows_q[key] = (codes, scales)
+
+        interleaved = {}
+
+        def raw_block(name, jp, g):
+            words = w_raw[(name, jp // 2)][:].rearrange("c (g t n) -> c g t n", g=PASSES, t=PACK)
+            return words[:, g, :, jp % 2 * BLOCK : (jp % 2 + 1) * BLOCK]
+
+        def interleave(name, jp, g):
+            bank = inter_pool.tile([P, BLOCK * PACK], BF16, tag="inter", name="interleaved")
+            out = bank[:].rearrange("c (n t) -> c t n", t=PACK)
+            for t in range(PACK):
+                nc.tensor.matmul(
+                    out=out[:, t],
+                    lhsT=ident_b[:],
+                    rhs=raw_block(name, jp, g)[:, t, :].rearrange("c (n u) -> c u n", u=UNITS),
+                    start=True,
+                    stop=True,
+                )
+            interleaved[(name, jp, g)] = bank
 
         def group_weight(name, jp, g, copy):
-            raw = w_raw[(name, jp // 2)]
-            if (name, jp) not in grouped_of:
-                grouped_of[(name, jp)] = w_grouped_pool.tile(
+            key = (name, jp)
+            if key not in grouped_of:
+                grouped_of[key] = w_grouped_pool.tile(
                     [P, PASSES * BLOCK * PACK], BF16, tag="w_grouped", align_bytes=64, name="grouped_w"
                 )
-            dst = grouped_of[(name, jp)][:, g * BLOCK * PACK : (g + 1) * BLOCK * PACK]
-            copy(
-                out=dst.rearrange("c (u n i t) -> c n t i u", u=UNITS, i=2, t=PACK),
-                in_=raw[:, g * PACK : (g + 1) * PACK, jp % 2 * BLOCK : (jp % 2 + 1) * BLOCK].rearrange(
-                    "c t (n i u) -> c n t i u", u=UNITS, i=2
-                ),
-            )
+            dst = grouped_of[key][:, g * BLOCK * PACK : (g + 1) * BLOCK * PACK]
+            if (name, jp, g) in interleaved:
+                copy(out=dst, in_=interleaved[(name, jp, g)][:])
+            else:
+                copy(
+                    out=dst.rearrange("c (u n i t) -> c n t i u", u=UNITS, i=2, t=PACK),
+                    in_=raw_block(name, jp, g).rearrange("c t (n i u) -> c n t i u", u=UNITS, i=2),
+                )
+            chunk = (name, jp // 2)
+            readers_left[chunk] = readers_left[chunk] - 1
+            if readers_left[chunk] == 0:
+                load_next_weight()
 
-        def quantise_weight(key):
-            grouped = grouped_of[key]
+        def quantise_weight(name, jp):
             codes = w_q_pool.tile([P, PASSES * BLOCK], U32, tag="w_codes", align_bytes=64, name="codes_w")
             scales = w_q_pool.tile([P, PASSES * BLOCK], U8, tag="w_scales", align_bytes=64, name="scales_w")
-            nc.vector.quantize_mx(out=codes[:].bitcast(FP8X4), scales=scales[:], in_=grouped[:])
-            w_q[key] = (codes, scales)
+            nc.vector.quantize_mx(out=codes[:].bitcast(FP8X4), scales=scales[:], in_=grouped_of[(name, jp)][:])
+            w_q[(name, jp)] = (codes, scales)
 
-        def add_passes(acc, weight_q, u, moving_q, first, last):
-            w_codes, w_scales = weight_q
+        def add_passes(acc, name, jp, u, moving_q, first, last):
             r_codes, r_scales = moving_q
             for g in range(PASSES):
+                w_codes, w_scales = w_q[(name, jp)]
                 m_cols = slice(g * BLOCK + u * P, g * BLOCK + (u + 1) * P)
                 n_cols = slice(g * ROWS, (g + 1) * ROWS)
                 nc.tensor.matmul_mx(
@@ -208,25 +240,19 @@ def tile_relationalmemorycorecell_pa_kernel(
             banks = {}
             for u in range(UNITS):
                 acc = acc_pool.tile([P, ROWS], F32, tag="acc", name="acc_gate")
-                add_passes(acc, w_q[(PHASE_WEIGHTS[kind][1], jp)], u, rows_q[("x", 0)], True, False)
+                add_passes(acc, PHASE_WEIGHTS[kind][1], jp, u, rows_q[("x", 0)], True, False)
                 banks[("gate", u)] = acc
             return banks
 
         def multiply_rows(step, banks):
             kind, jp, r = step
-            names = PHASE_WEIGHTS[kind]
             for u in range(UNITS):
-                add_passes(banks[("gate", u)], w_q[(names[0], jp)], u, rows_q[("h", r)], False, True)
+                add_passes(banks[("gate", u)], PHASE_WEIGHTS[kind][0], jp, u, rows_q[("h", r)], False, True)
             if kind == "ig":
                 for u in range(UNITS):
                     acc = acc_pool.tile([P, ROWS], F32, tag="acc", name="acc_prop")
-                    add_passes(acc, w_q[("g", jp)], u, rows_q[("p", r)], True, True)
+                    add_passes(acc, "g", jp, u, rows_q[("p", r)], True, True)
                     banks[("prop", u)] = acc
-
-        def multiply(step):
-            banks = multiply_inputs(step)
-            multiply_rows(step, banks)
-            return banks
 
         def activate(step, banks):
             kind, jp, r = step
@@ -239,15 +265,9 @@ def tile_relationalmemorycorecell_pa_kernel(
             if kind != "f":
                 nc.scalar.activation(out=gate[:], in_=gate[:], func=ACT.Sigmoid)
             tiles["gate"] = gate
-            if kind == "o":
-                tanh_m = work.tile([P, GROUP_SLOTS, BLOCK], F32, tag="tanh", bufs=2, name="tanh_m")
-                nc.scalar.activation(
-                    out=tanh_m[:], in_=m_blocks[jp][:, r * GROUP_SLOTS : (r + 1) * GROUP_SLOTS, :], func=ACT.Tanh
-                )
-                tiles["tanh"] = tanh_m
             if kind == "ig":
                 prop = work.tile([P, UNITS, ROWS], F32, tag="prop", bufs=2, name="prop")
-                p_view = grouped_of[("p", r)][0][:].rearrange("c (g w t) -> c g w t", g=PASSES, w=ROWS, t=PACK)
+                p_view = grouped_of[("p", r)][:].rearrange("c (g w t) -> c g w t", g=PASSES, w=ROWS, t=PACK)
                 for u in range(UNITS):
                     nc.vector.scalar_tensor_tensor(
                         out=prop[:, u, :],
@@ -259,6 +279,13 @@ def tile_relationalmemorycorecell_pa_kernel(
                     )
                 tiles["prop"] = prop
             return tiles
+
+        def squash(step, tiles):
+            kind, jp, r = step
+            if kind == "o":
+                tanh_m = work.tile([P, GROUP_SLOTS, BLOCK], F32, tag="tanh", bufs=2, name="tanh_m")
+                nc.scalar.activation(out=tanh_m[:], in_=m_block(jp, r), func=ACT.Tanh)
+                tiles["tanh"] = tanh_m
 
         def weigh(step, tiles):
             if step[0] == "ig":
@@ -277,9 +304,8 @@ def tile_relationalmemorycorecell_pa_kernel(
 
         kept = {}
 
-        def finish(step, tiles):
+        def combine(step, tiles):
             kind, jp, r = step
-            slots = slice(r * GROUP_SLOTS, (r + 1) * GROUP_SLOTS)
             features = slice(jp * BLOCK, (jp + 1) * BLOCK)
             if kind == "ig":
                 out_tile = kept[(jp, r)]
@@ -287,17 +313,20 @@ def tile_relationalmemorycorecell_pa_kernel(
                 out_tile = work.tile([P, GROUP_SLOTS, BLOCK], F32, tag="out_" + kind, bufs=OUT_BUFS[kind], name="out_" + kind)
             for v in range(UNITS):
                 pair = slice(v * SLOT_PAIR, (v + 1) * SLOT_PAIR)
-                other = {"o": tiles.get("tanh"), "f": m_blocks[jp][:, slots, :], "ig": out_tile}[kind]
+                other = {"o": tiles.get("tanh"), "f": m_block(jp, r), "ig": out_tile}[kind]
                 nc.vector.tensor_tensor(
                     out=out_tile[:, pair, :].rearrange("b s (c u) -> b s c u", u=UNITS),
                     in0=tiles[("back", v)][:].rearrange("b s u c -> b s c u"),
                     in1=other[:, pair, :].rearrange("b s (c u) -> b s c u", u=UNITS),
                     op=(ALU.add if kind == "ig" else ALU.mult),
                 )
-            if kind == "f":
-                nc.scalar.activation(out=out_tile[:], in_=out_tile[:], func=ACT.Sigmoid, bias=1.0)
-                kept[(jp, r)] = out_tile
             tiles["out"] = out_tile
+
+        def finish(step, tiles):
+            kind, jp, r = step
+            if kind == "f":
+                nc.scalar.activation(out=tiles["out"][:], in_=tiles["out"][:], func=ACT.Sigmoid, bias=1.0)
+                kept[(jp, r)] = tiles["out"]
 
         def store(step, tiles):
             kind, jp, r = step
@@ -308,21 +337,49 @@ def tile_relationalmemorycorecell_pa_kernel(
             if kind == "ig":
                 nc.scalar.dma_start(out=out_0[:, slots, features], in_=tiles["out"][:])
 
+        tasks = list(TASKS)
+        waiting = []
+
+        def run_tasks(engines):
+            for letter in engines:
+                if not tasks:
+                    return
+                task = tasks.pop(0)
+                if task[0] == "slot":
+                    group_slot(task[1], task[2], task[3], SC if letter in "SP" else VC)
+                    if task[3] == GROUP_SLOTS - 1:
+                        waiting.append(task)
+                else:
+                    group_weight(task[1], task[2], task[3], COPY[letter])
+                    if task[3] == 1:
+                        waiting.append(task)
+
+        def interleave_tasks(engines, ahead):
+            for letter, task in zip(engines, tasks[ahead:]):
+                if letter == "P" and task[0] == "w" and (task[1], task[2], task[3]) not in interleaved:
+                    interleave(task[1], task[2], task[3])
+
+        def run_quantises():
+            while waiting:
+                task = waiting.pop(0)
+                if task[0] == "slot":
+                    quantise_rows((task[1], task[2]))
+                else:
+                    quantise_weight(task[1], task[2])
+
+        def ensure(step):
+            kind, jp, r = step
+            need = [(n, jp) for n in PHASE_WEIGHTS[kind]]
+            while any([k not in w_q for k in need]) or (kind == "ig" and ("p", r) not in rows_q):
+                if not waiting:
+                    run_tasks("V")
+                run_quantises()
+
         ctx.enter_context(tc.manual_schedule(engines=PINNED))
-        SC, VC = nc.scalar.copy, nc.vector.tensor_copy
-        H0 = [SC, SC, SC, SC]
-        H1 = [SC, VC, SC, VC]
-        WO = [VC, VC]
-        UO = [VC, SC]
-        UF = [(2, VC), (1, SC), (1, VC)]
         x_grouped = const.tile([P, WIDTH], BF16, align_bytes=64, name="grouped_x")
         nc.scalar.copy(
             out=x_grouped[:].bitcast(F32).rearrange("c (g b u) -> c g b u", g=PASSES, b=P, u=2), in_=flip_words(x_sb[:])
         )
-        bias_flipped = back_pool.tile([P, P], F32, tag="back", name="bias_flipped")
-        nc.tensor.transpose(bias_flipped[:], bias_rows[:].bitcast(F32), ident_f[:])
-        n_bias = len(BIAS_ORDER) * BLOCKS * UNITS
-        nc.vector.tensor_copy(out=bias_cols[:, 0:n_bias], in_=bias_flipped[:].bitcast(BF16)[:, 0:n_bias])
         x_codes = const.tile([P, PASSES, P], U32, align_bytes=64, name="x_codes")
         x_scales = const.tile([P, PASSES, P], U8, align_bytes=64, name="x_scales")
         nc.gpsimd.memset(x_scales[:].rearrange("c g b -> c (g b)").bitcast(I32), 0)
@@ -339,87 +396,82 @@ def tile_relationalmemorycorecell_pa_kernel(
                 in_=one[:].bitcast(I32).unsqueeze(2).to_broadcast([P, PASSES, GROUP_SLOTS, n]),
             )
         rows_q[("x", 0)] = (codes_x, scales_x)
+        first = PHASE_WEIGHTS[PHASES[0][0]]
         for g in range(PASSES):
-            group_weight("wo", 0, g, WO[g])
-        quantise_weight(("wo", 0))
+            group_weight(first[1], 0, g, COPY[HEAD["w"][g]])
+        quantise_weight(first[1], 0)
         for g in range(PASSES):
-            group_weight("uo", 0, g, UO[g])
+            group_weight(first[0], 0, g, COPY[HEAD["u"][g]])
         for s in range(GROUP_SLOTS):
-            group_slot("h", 0, s, H0[s])
+            group_slot("h", 0, s, COPY[HEAD["h0"][s]])
         banks = multiply_inputs(steps[0])
-        quantise_weight(("uo", 0))
+        quantise_weight(first[0], 0)
         quantise_rows(("h", 0))
-        tasks = []
-        for kind, jp in phases:
-            if (kind, jp) == ("ig", 0):
-                for r in range(ROW_GROUPS):
-                    tasks.extend([("slot", ("p", r), s) for s in range(GROUP_SLOTS)])
-            for name in PHASE_WEIGHTS[kind]:
-                if (kind, jp) != ("o", 0):
-                    tasks.extend([("half", (name, jp), g) for g in range(PASSES)])
-        waiting = []
-
-        def run_tasks(count, weight_copy, slot_copy):
-            for what, key, part in tasks[:count]:
-                if what == "half":
-                    group_weight(key[0], key[1], part, weight_copy)
-                    if part == PASSES - 1:
-                        waiting.append((what, key))
-                        if key[1] % 2 == 1:
-                            load_next_weight()
-                else:
-                    group_slot(key[0], key[1], part, slot_copy)
-                    if part == GROUP_SLOTS - 1:
-                        waiting.append((what, key))
-            for task in tasks[:count]:
-                tasks.remove(task)
-
-        def run_quantises():
-            for what, key in waiting:
-                if what == "half":
-                    quantise_weight(key)
-                else:
-                    quantise_rows(key)
-            waiting.clear()
-
-        def gpsimd_copy(out, in_):
-            nc.gpsimd.tensor_scalar(out=out, in0=in_, scalar1=1.0, scalar2=0.0, op0=ALU.mult, op1=ALU.add)
-
-        def ensure(step):
-            kind, jp, r = step
-            keys = [(n, jp) for n in PHASE_WEIGHTS[kind]]
-            while any([k not in w_q for k in keys]) or (kind == "ig" and ("p", r) not in rows_q):
-                if not waiting:
-                    run_tasks(1, nc.vector.tensor_copy, nc.scalar.copy)
-                run_quantises()
-
-        for count, copy in UF[0:1]:
-            run_tasks(count, copy, copy)
+        bias_flipped = back_pool.tile([P, P], F32, tag="back", name="bias_flipped")
+        nc.tensor.transpose(bias_flipped[:], bias_rows[:].bitcast(F32), ident_f[:])
+        n_bias = len(BIAS_ORDER) * BLOCKS * UNITS
+        nc.vector.tensor_copy(out=bias_cols[:, 0:n_bias], in_=bias_flipped[:].bitcast(BF16)[:, 0:n_bias])
+        run_tasks(HEAD["t0"])
         run_quantises()
         multiply_rows(steps[0], banks)
         for s in range(GROUP_SLOTS):
-            group_slot("h", 1, s, H1[s])
+            group_slot("h", 1, s, COPY[HEAD["h1"][s]])
+        run_tasks(HEAD["t1"])
         quantise_rows(("h", 1))
-        for count, copy in UF[1:]:
-            run_tasks(count, copy, copy)
+        run_tasks(HEAD["t2"])
+
         tiles_of = {}
-        for i, step in enumerate(steps):
-            tiles_of[i] = activate(step, banks)
-            if i >= 1:
-                flip_back(steps[i - 1], tiles_of[i - 1])
+
+        def do_multiply(i):
             if i + 1 < len(steps):
                 ensure(steps[i + 1])
-                banks = multiply(steps[i + 1])
-            if i >= 1:
-                finish(steps[i - 1], tiles_of[i - 1])
+                banks = multiply_inputs(steps[i + 1])
+                multiply_rows(steps[i + 1], banks)
+                return banks
+            return {}
+
+        def do_tasks(i):
             run_quantises()
-            for_vector, for_scalar, for_gpsimd = (SHARES[step[0]][step[2]] + (0,))[:3]
-            run_tasks(for_vector, nc.vector.tensor_copy, nc.vector.tensor_copy)
-            run_tasks(for_scalar, nc.scalar.copy, nc.scalar.copy)
-            run_tasks(for_gpsimd, gpsimd_copy, nc.vector.tensor_copy)
+            run_tasks(SHARES[steps[i][0]][i % len(SHARES[steps[i][0]])])
+
+        for i, step in enumerate(steps):
+            tiles_of[i] = activate(step, banks)
+            pe_first = "A" if MULT_FIRST[step[0]] else "D"
+            if pe_first == "A":
+                banks = do_multiply(i)
             if i >= 1:
+                flip_back(steps[i - 1], tiles_of[i - 1])
+            if pe_first == "D":
+                banks = do_multiply(i)
+            if i + 1 < len(steps):
+                if i == 0:
+                    interleave_tasks(SHARES[step[0]][0], 0)
+                ahead = len(SHARES[step[0]][i % len(SHARES[step[0]])])
+                interleave_tasks(SHARES[steps[i + 1][0]][(i + 1) % len(SHARES[steps[i + 1][0]])], ahead)
+            if FINISH_LATE and i >= 2:
+                finish(steps[i - 2], tiles_of[i - 2])
+            if TANH_EARLY:
+                squash(step, tiles_of[i])
+            if TASKS_FIRST[step[0]]:
+                do_tasks(i)
+            if i >= 1:
+                combine(steps[i - 1], tiles_of[i - 1])
+            if not FINISH_LATE and i >= 1:
+                finish(steps[i - 1], tiles_of[i - 1])
+            if not TASKS_FIRST[step[0]]:
+                do_tasks(i)
+            if not TANH_EARLY:
+                squash(step, tiles_of[i])
+            if FINISH_LATE and i >= 2:
+                store(steps[i - 2], tiles_of[i - 2])
+            if not FINISH_LATE and i >= 1:
                 store(steps[i - 1], tiles_of[i - 1])
             weigh(step, tiles_of[i])
-        flip_back(steps[-1], tiles_of[len(steps) - 1])
-        finish(steps[-1], tiles_of[len(steps) - 1])
-        store(steps[-1], tiles_of[len(steps) - 1])
+        last = len(steps) - 1
+        flip_back(steps[last], tiles_of[last])
+        if FINISH_LATE:
+            finish(steps[last - 1], tiles_of[last - 1])
+            store(steps[last - 1], tiles_of[last - 1])
+        combine(steps[last], tiles_of[last])
+        finish(steps[last], tiles_of[last])
+        store(steps[last], tiles_of[last])

@@ -30,22 +30,20 @@ FLOPS = 2 * P * SLOTS * WIDTH * WIDTH * 4 + 2 * P * WIDTH * WIDTH * 3
 
 PHASE_WEIGHTS = {"o": ("uo", "wo"), "f": ("uf", "wf"), "ig": ("ui", "wi", "g")}
 BIAS_ORDER = ("g", "f", "i", "o")
-PHASES = [("o", 0), ("o", 1), ("f", 0), ("f", 1), ("o", 2), ("o", 3), ("ig", 0), ("ig", 1), ("f", 2), ("f", 3), ("ig", 2), ("ig", 3)]
-LOADS = [("x", 0), ("wo", 0, 0, 512), ("uo", 0, 0, 512), ("h", 0), ("h", 1), ("m", 0, 0), ("m", 1, 0), ("uf", 0, 0, 512), ("wf", 0, 0, 512), ("uo", 1, 0, 512), ("wo", 1, 0, 512), ("m", 0, 1), ("m", 1, 1), ("p", 0), ("p", 1), ("ui", 0, 0, 512), ("wi", 0, 0, 512), ("g", 0, 0, 512), ("uf", 1, 0, 512), ("wf", 1, 0, 512), ("ui", 1, 0, 512), ("wi", 1, 0, 512), ("g", 1, 0, 512)]
-TASKS = [("w", "uo", 1, 0), ("w", "uo", 1, 1), ("w", "wo", 1, 0), ("w", "wo", 1, 1), ("w", "uf", 0, 0), ("w", "uf", 0, 1), ("w", "wf", 0, 0), ("w", "wf", 0, 1), ("w", "uf", 1, 0), ("w", "uf", 1, 1), ("w", "wf", 1, 0), ("w", "wf", 1, 1), ("w", "uo", 2, 0), ("w", "uo", 2, 1), ("w", "wo", 2, 0), ("w", "wo", 2, 1), ("w", "uo", 3, 0), ("w", "uo", 3, 1), ("w", "wo", 3, 0), ("w", "wo", 3, 1), ("slot", "p", 0, 0), ("slot", "p", 0, 1), ("slot", "p", 0, 2), ("slot", "p", 0, 3), ("slot", "p", 1, 0), ("slot", "p", 1, 1), ("slot", "p", 1, 2), ("slot", "p", 1, 3), ("w", "ui", 0, 0), ("w", "ui", 0, 1), ("w", "wi", 0, 0), ("w", "wi", 0, 1), ("w", "g", 0, 0), ("w", "g", 0, 1), ("w", "ui", 1, 0), ("w", "ui", 1, 1), ("w", "wi", 1, 0), ("w", "wi", 1, 1), ("w", "g", 1, 0), ("w", "g", 1, 1), ("w", "uf", 2, 0), ("w", "uf", 2, 1), ("w", "wf", 2, 0), ("w", "wf", 2, 1), ("w", "uf", 3, 0), ("w", "uf", 3, 1), ("w", "wf", 3, 0), ("w", "wf", 3, 1), ("w", "ui", 2, 0), ("w", "ui", 2, 1), ("w", "wi", 2, 0), ("w", "wi", 2, 1), ("w", "g", 2, 0), ("w", "g", 2, 1), ("w", "ui", 3, 0), ("w", "ui", 3, 1), ("w", "wi", 3, 0), ("w", "wi", 3, 1), ("w", "g", 3, 0), ("w", "g", 3, 1)]
-SHARES = {"o":["VVV"],"f":["VVSS","VVVS"],"ig":["S"]}
-HEAD = {"w":"VV","u":"VS","h0":"SSSS","h1":"SVSV","t0":"VV","t1":"","t2":"SV"}
+PHASES = [("o", 0), ("o", 1), ("f", 0), ("o", 2), ("f", 1), ("ig", 0), ("o", 3), ("ig", 1), ("f", 2), ("f", 3), ("ig", 2), ("ig", 3)]
+LOADS = [("x", 0), ("wo", "k", 0), ("wo", "k", 1), ("h", 0), ("uo", "k", 0), ("uo", "k", 1), ("h", 1), ("m", 0, 0), ("m", 1, 0), ("uf", "n", 0), ("wf", "n", 0), ("m", 0, 1), ("m", 1, 1), ("p", 0), ("p", 1), ("ui", "n", 0), ("wi", "n", 0), ("g", "n", 0), ("uf", "n", 1), ("wf", "n", 1), ("ui", "n", 1), ("wi", "n", 1), ("g", "n", 1)]
+TASKS = [("w", "wo", 0, 0), ("w", "wo", 1, 0), ("w", "wo", 2, 0), ("w", "wo", 3, 0), ("w", "wo", 0, 1), ("w", "wo", 1, 1), ("w", "wo", 2, 1), ("w", "wo", 3, 1), ("w", "uo", 0, 0), ("w", "uo", 1, 0), ("w", "uo", 2, 0), ("w", "uo", 3, 0), ("w", "uo", 0, 1), ("w", "uo", 1, 1), ("w", "uo", 2, 1), ("w", "uo", 3, 1), ("w", "uf", 0, 0), ("w", "uf", 0, 1), ("w", "wf", 0, 0), ("w", "wf", 0, 1), ("w", "uf", 1, 0), ("w", "uf", 1, 1), ("w", "wf", 1, 0), ("w", "wf", 1, 1), ("slot", "p", 0, 0), ("slot", "p", 0, 1), ("slot", "p", 0, 2), ("slot", "p", 0, 3), ("slot", "p", 1, 0), ("slot", "p", 1, 1), ("slot", "p", 1, 2), ("slot", "p", 1, 3), ("w", "ui", 0, 0), ("w", "ui", 0, 1), ("w", "wi", 0, 0), ("w", "wi", 0, 1), ("w", "g", 0, 0), ("w", "g", 0, 1), ("w", "ui", 1, 0), ("w", "ui", 1, 1), ("w", "wi", 1, 0), ("w", "wi", 1, 1), ("w", "g", 1, 0), ("w", "g", 1, 1), ("w", "uf", 2, 0), ("w", "uf", 2, 1), ("w", "wf", 2, 0), ("w", "wf", 2, 1), ("w", "uf", 3, 0), ("w", "uf", 3, 1), ("w", "wf", 3, 0), ("w", "wf", 3, 1), ("w", "ui", 2, 0), ("w", "ui", 2, 1), ("w", "wi", 2, 0), ("w", "wi", 2, 1), ("w", "g", 2, 0), ("w", "g", 2, 1), ("w", "ui", 3, 0), ("w", "ui", 3, 1), ("w", "wi", 3, 0), ("w", "wi", 3, 1), ("w", "g", 3, 0), ("w", "g", 3, 1)]
+SHARES = {"o":["VVV","VV"],"f":["VVSS","SVV"],"ig":["S","S"]}
+HEAD = [("w", "wo", 0, 0, "V"), ("w", "wo", 1, 0, "V"), ("w", "wo", 2, 0, "S"), ("w", "wo", 3, 0, "S"), ("w", "wo", 0, 1, "V"), ("q", "wo", 0), ("w", "wo", 1, 1, "V"), ("q", "wo", 1), ("w", "wo", 2, 1, "S"), ("w", "wo", 3, 1, "V"), ("h", 0, "SSSS"), ("q", "wo", 2), ("q", "wo", 3), ("qh", 0), ("w", "uo", 0, 0, "V"), ("w", "uo", 1, 0, "V"), ("w", "uo", 2, 0, "S"), ("w", "uo", 3, 0, "S"), ("mx", 0), ("w", "uo", 0, 1, "V"), ("q", "uo", 0), ("b", 0), ("mh", 0), ("w", "uo", 1, 1, "V"), ("q", "uo", 1), ("h", 1, "SSSS"), ("w", "uo", 2, 1, "V"), ("q", "uo", 2), ("w", "uo", 3, 1, "V"), ("q", "uo", 3), ("qh", 1)]
 W_RAW_BUFS = 5
-SPLIT_LOADS = 0
-W_Q_BUFS = 9
-GROUPED_BUFS = 4
-OUT_BUFS = {"o":3,"f":7}
+W_Q_BUFS = 12
+GROUPED_BUFS = 5
+OUT_BUFS = {"o":3,"f":6}
 ACC_BUFS = 4
-INTER_BUFS = 0
 TANH_EARLY = False
 FINISH_LATE = True
 MULT_FIRST = {"o": True, "f": True, "ig": False}
-TASKS_FIRST = {"o": True, "f": True, "ig": True}
+TASKS_FIRST = {"o": True, "f": True, "ig": False}
 PINNED = {mybir.EngineType.PE, mybir.EngineType.DVE, mybir.EngineType.Activation}
 
 
@@ -72,19 +70,17 @@ def tile_relationalmemorycorecell_pa_kernel(
         w_q_pool = ctx.enter_context(tc.tile_pool(name="w_q", bufs=W_Q_BUFS))
         work = ctx.enter_context(tc.tile_pool(name="work", bufs=3))
         acc_pool = ctx.enter_context(tc.psum_pool(name="acc", bufs=ACC_BUFS))
-        back_pool = ctx.enter_context(tc.psum_pool(name="back", bufs=8 - ACC_BUFS - INTER_BUFS))
-        inter_pool = ctx.enter_context(tc.psum_pool(name="inter", bufs=INTER_BUFS)) if INTER_BUFS > 0 else back_pool
+        back_pool = ctx.enter_context(tc.psum_pool(name="back", bufs=8 - ACC_BUFS))
 
         ident_f = const.tile([P, P], F32, name="ident_f")
         make_identity(nc, ident_f[:])
-        ident_b = const.tile([P, P], BF16, name="ident_b")
-        make_identity(nc, ident_b[:])
 
         x_sb = const.tile([P, WIDTH], BF16, name="x_sb")
         rows_raw = {}
         m_rows = {}
         w_raw = {}
         readers_left = {}
+        chunk_of = {}
 
         def load_rows(name, r):
             raw = rows_pool.tile([P, GROUP_SLOTS * WIDTH], BF16, tag="rows_raw", name="raw_" + name)
@@ -106,15 +102,27 @@ def tile_relationalmemorycorecell_pa_kernel(
         def m_block(jp, r):
             return m_rows[(r, jp // 2)][:, :, jp % 2 * BLOCK : (jp % 2 + 1) * BLOCK]
 
-        def load_weight(name, k, first, last):
-            if (name, k) not in w_raw:
-                raw = w_raw_pool.tile([P, 2 * PACK * HALF], BF16, tag="w_raw", name="raw_" + name)
-                w_raw[(name, k)] = raw
-                readers_left[(name, k)] = 4
-            dst = w_raw[(name, k)][:].rearrange("c (a e n) -> c a e n", e=2, n=HALF)[:, :, :, first:last]
-            src = weight_of[name][:, k * HALF + first : k * HALF + last].rearrange("(a c e) n -> c a e n", c=P, e=2)
-            for e in range(2):
-                nc.sync.dma_start(out=dst[:, :, e, :], in_=src[:, :, e, :])
+        def load_weight(name, how, k):
+            raw = w_raw_pool.tile([P, 2 * PACK * HALF], BF16, tag="w_raw", name="raw_" + name)
+            readers_left[(name, how, k)] = 4
+            if how == "n":
+                dst = raw[:].rearrange("c (a e n) -> c a e n", e=2, n=HALF)
+                src = weight_of[name][:, k * HALF : (k + 1) * HALF].rearrange("(a c e) n -> c a e n", c=P, e=2)
+                for e in range(2):
+                    nc.sync.dma_start(out=dst[:, :, e, :], in_=src[:, :, e, :])
+                words = raw[:].rearrange("c (g t n) -> c g t n", g=PASSES, t=PACK)
+                for g in range(PASSES):
+                    w_raw[(name, k, g)] = words[:, g]
+                    chunk_of[(name, k, g)] = (name, how, k)
+            else:
+                src = weight_of[name][k * P * PACK : (k + 1) * P * PACK, :]
+                nc.sync.dma_start(
+                    out=raw[:].rearrange("c (u m) -> c u m", u=2), in_=src.rearrange("(u c e) n -> c u (e n)", c=P, e=2)
+                )
+                words = raw[:].rearrange("c (t n) -> c t n", t=PACK)
+                for half in range(2):
+                    w_raw[(name, half, k)] = words[:, :, half * HALF : (half + 1) * HALF]
+                    chunk_of[(name, half, k)] = (name, how, k)
 
         loads = list(LOADS)
 
@@ -124,7 +132,7 @@ def tile_relationalmemorycorecell_pa_kernel(
                 load = loads.pop(0)
                 seen = seen or load[0] in weight_of
                 if load[0] in weight_of:
-                    load_weight(load[0], load[1], load[2], load[3])
+                    load_weight(load[0], load[1], load[2])
                 elif load[0] == "m":
                     load_m(load[1], load[2])
                 elif load[0] == "x":
@@ -132,7 +140,7 @@ def tile_relationalmemorycorecell_pa_kernel(
                 else:
                     load_rows(load[0], load[1])
 
-        for count in range(W_RAW_BUFS + SPLIT_LOADS):
+        for count in range(W_RAW_BUFS):
             load_next_weight()
 
         bias_rows = const.tile([P, BLOCK], BF16, name="bias_rows")
@@ -159,6 +167,11 @@ def tile_relationalmemorycorecell_pa_kernel(
                 nc.tensor.transpose(flipped[:, a * P : (a + 1) * P], words[:, a * P : (a + 1) * P], ident_f[:])
             return flipped[:].rearrange("c (g u b) -> c g b u", g=PASSES, u=2, b=P)
 
+        flipped_of = {}
+
+        def flip_slot(name, r, s):
+            flipped_of[(name, r, s)] = flip_words(rows_raw[(name, r)][:, s * WIDTH : (s + 1) * WIDTH])
+
         def group_slot(name, r, s, copy):
             if (name, r) not in grouped_of:
                 grouped_of[(name, r)] = rows_pool.tile(
@@ -167,7 +180,9 @@ def tile_relationalmemorycorecell_pa_kernel(
             view = grouped_of[(name, r)][:].bitcast(F32).rearrange(
                 "c (g s b u) -> c g s b u", g=PASSES, s=GROUP_SLOTS, b=P, u=2
             )
-            copy(out=view[:, :, s, :, :], in_=flip_words(rows_raw[(name, r)][:, s * WIDTH : (s + 1) * WIDTH]))
+            if (name, r, s) not in flipped_of:
+                flip_slot(name, r, s)
+            copy(out=view[:, :, s, :, :], in_=flipped_of[(name, r, s)])
 
         def quantise_rows(key):
             codes = const.tile([P, PASSES * ROWS], U32, align_bytes=64, name="codes_%s%d" % key)
@@ -175,24 +190,8 @@ def tile_relationalmemorycorecell_pa_kernel(
             nc.vector.quantize_mx(out=codes[:].bitcast(FP8X4), scales=scales[:], in_=grouped_of[key][:])
             rows_q[key] = (codes, scales)
 
-        interleaved = {}
-
         def raw_block(name, jp, g):
-            words = w_raw[(name, jp // 2)][:].rearrange("c (g t n) -> c g t n", g=PASSES, t=PACK)
-            return words[:, g, :, jp % 2 * BLOCK : (jp % 2 + 1) * BLOCK]
-
-        def interleave(name, jp, g):
-            bank = inter_pool.tile([P, BLOCK * PACK], BF16, tag="inter", name="interleaved")
-            out = bank[:].rearrange("c (n t) -> c t n", t=PACK)
-            for t in range(PACK):
-                nc.tensor.matmul(
-                    out=out[:, t],
-                    lhsT=ident_b[:],
-                    rhs=raw_block(name, jp, g)[:, t, :].rearrange("c (n u) -> c u n", u=UNITS),
-                    start=True,
-                    stop=True,
-                )
-            interleaved[(name, jp, g)] = bank
+            return w_raw[(name, jp // 2, g)][:, :, jp % 2 * BLOCK : (jp % 2 + 1) * BLOCK]
 
         def group_weight(name, jp, g, copy):
             key = (name, jp)
@@ -201,14 +200,11 @@ def tile_relationalmemorycorecell_pa_kernel(
                     [P, PASSES * BLOCK * PACK], BF16, tag="w_grouped", align_bytes=64, name="grouped_w"
                 )
             dst = grouped_of[key][:, g * BLOCK * PACK : (g + 1) * BLOCK * PACK]
-            if (name, jp, g) in interleaved:
-                copy(out=dst, in_=interleaved[(name, jp, g)][:])
-            else:
-                copy(
-                    out=dst.rearrange("c (u n i t) -> c n t i u", u=UNITS, i=2, t=PACK),
-                    in_=raw_block(name, jp, g).rearrange("c t (n i u) -> c n t i u", u=UNITS, i=2),
-                )
-            chunk = (name, jp // 2)
+            copy(
+                out=dst.rearrange("c (u n i t) -> c n t i u", u=UNITS, i=2, t=PACK),
+                in_=raw_block(name, jp, g).rearrange("c t (n i u) -> c n t i u", u=UNITS, i=2),
+            )
+            chunk = chunk_of[(name, jp // 2, g)]
             readers_left[chunk] = readers_left[chunk] - 1
             if readers_left[chunk] == 0:
                 load_next_weight()
@@ -262,7 +258,7 @@ def tile_relationalmemorycorecell_pa_kernel(
                 nc.scalar.activation(
                     out=gate[:, u, :], in_=banks[("gate", u)][:], func=ACT.Sigmoid, bias=bias_col(kind[0], jp, u)
                 )
-            if kind != "f":
+            if kind != "f" and step != steps[-1]:
                 nc.scalar.activation(out=gate[:], in_=gate[:], func=ACT.Sigmoid)
             tiles["gate"] = gate
             if kind == "ig":
@@ -288,7 +284,7 @@ def tile_relationalmemorycorecell_pa_kernel(
                 tiles["tanh"] = tanh_m
 
         def weigh(step, tiles):
-            if step[0] == "ig":
+            if step[0] == "ig" and step != steps[-1]:
                 prop = tiles["prop"]
                 nc.vector.tensor_tensor(out=prop[:], in0=prop[:], in1=tiles["gate"][:], op=ALU.mult)
 
@@ -338,6 +334,7 @@ def tile_relationalmemorycorecell_pa_kernel(
                 nc.scalar.dma_start(out=out_0[:, slots, features], in_=tiles["out"][:])
 
         tasks = list(TASKS)
+        halves_done = {}
         waiting = []
 
         def run_tasks(engines):
@@ -351,13 +348,9 @@ def tile_relationalmemorycorecell_pa_kernel(
                         waiting.append(task)
                 else:
                     group_weight(task[1], task[2], task[3], COPY[letter])
-                    if task[3] == 1:
+                    halves_done[(task[1], task[2])] = halves_done.get((task[1], task[2]), 0) + 1
+                    if halves_done[(task[1], task[2])] == PASSES:
                         waiting.append(task)
-
-        def interleave_tasks(engines, ahead):
-            for letter, task in zip(engines, tasks[ahead:]):
-                if letter == "P" and task[0] == "w" and (task[1], task[2], task[3]) not in interleaved:
-                    interleave(task[1], task[2], task[3])
 
         def run_quantises():
             while waiting:
@@ -396,31 +389,34 @@ def tile_relationalmemorycorecell_pa_kernel(
                 in_=one[:].bitcast(I32).unsqueeze(2).to_broadcast([P, PASSES, GROUP_SLOTS, n]),
             )
         rows_q[("x", 0)] = (codes_x, scales_x)
-        first = PHASE_WEIGHTS[PHASES[0][0]]
-        for g in range(PASSES):
-            group_weight(first[1], 0, g, COPY[HEAD["w"][g]])
-        quantise_weight(first[1], 0)
-        for g in range(PASSES):
-            group_weight(first[0], 0, g, COPY[HEAD["u"][g]])
-        for s in range(GROUP_SLOTS):
-            group_slot("h", 0, s, COPY[HEAD["h0"][s]])
-        banks = multiply_inputs(steps[0])
-        quantise_weight(first[0], 0)
-        quantise_rows(("h", 0))
-        bias_flipped = back_pool.tile([P, P], F32, tag="back", name="bias_flipped")
-        nc.tensor.transpose(bias_flipped[:], bias_rows[:].bitcast(F32), ident_f[:])
-        n_bias = len(BIAS_ORDER) * BLOCKS * UNITS
-        nc.vector.tensor_copy(out=bias_cols[:, 0:n_bias], in_=bias_flipped[:].bitcast(BF16)[:, 0:n_bias])
-        run_tasks(HEAD["t0"])
-        run_quantises()
-        multiply_rows(steps[0], banks)
-        for s in range(GROUP_SLOTS):
-            group_slot("h", 1, s, COPY[HEAD["h1"][s]])
-        run_tasks(HEAD["t1"])
-        quantise_rows(("h", 1))
-        run_tasks(HEAD["t2"])
+        banks = {}
+        for op in HEAD:
+            if op[0] == "w":
+                group_weight(op[1], op[2], op[3], COPY[op[4]])
+                tasks.remove(("w", op[1], op[2], op[3]))
+                halves_done[(op[1], op[2])] = halves_done.get((op[1], op[2]), 0) + 1
+            elif op[0] == "q":
+                quantise_weight(op[1], op[2])
+            elif op[0] == "h":
+                for s in range(GROUP_SLOTS):
+                    group_slot("h", op[1], s, COPY[op[2][s]])
+            elif op[0] == "qh":
+                quantise_rows(("h", op[1]))
+            elif op[0] == "mx":
+                banks = multiply_inputs(steps[0])
+            elif op[0] == "mh":
+                multiply_rows(steps[0], banks)
+            elif op[0] == "b":
+                bias_flipped = back_pool.tile([P, P], F32, tag="back", name="bias_flipped")
+                nc.tensor.transpose(bias_flipped[:], bias_rows[:].bitcast(F32), ident_f[:])
+                n_bias = len(BIAS_ORDER) * BLOCKS * UNITS
+                nc.vector.tensor_copy(out=bias_cols[:, 0:n_bias], in_=bias_flipped[:].bitcast(BF16)[:, 0:n_bias])
 
         tiles_of = {}
+
+        def share_of(i):
+            shares = SHARES[steps[i][0]]
+            return shares[i % len(shares)]
 
         def do_multiply(i):
             if i + 1 < len(steps):
@@ -432,7 +428,7 @@ def tile_relationalmemorycorecell_pa_kernel(
 
         def do_tasks(i):
             run_quantises()
-            run_tasks(SHARES[steps[i][0]][i % len(SHARES[steps[i][0]])])
+            run_tasks(share_of(i))
 
         for i, step in enumerate(steps):
             tiles_of[i] = activate(step, banks)
@@ -444,10 +440,10 @@ def tile_relationalmemorycorecell_pa_kernel(
             if pe_first == "D":
                 banks = do_multiply(i)
             if i + 1 < len(steps):
-                if i == 0:
-                    interleave_tasks(SHARES[step[0]][0], 0)
-                ahead = len(SHARES[step[0]][i % len(SHARES[step[0]])])
-                interleave_tasks(SHARES[steps[i + 1][0]][(i + 1) % len(SHARES[steps[i + 1][0]])], ahead)
+                ahead = len(share_of(i))
+                for task in tasks[ahead : ahead + len(share_of(i + 1))]:
+                    if task[0] == "slot":
+                        flip_slot(task[1], task[2], task[3])
             if FINISH_LATE and i >= 2:
                 finish(steps[i - 2], tiles_of[i - 2])
             if TANH_EARLY:
@@ -467,11 +463,28 @@ def tile_relationalmemorycorecell_pa_kernel(
             if not FINISH_LATE and i >= 1:
                 store(steps[i - 1], tiles_of[i - 1])
             weigh(step, tiles_of[i])
-        last = len(steps) - 1
-        flip_back(steps[last], tiles_of[last])
-        if FINISH_LATE:
-            finish(steps[last - 1], tiles_of[last - 1])
-            store(steps[last - 1], tiles_of[last - 1])
-        combine(steps[last], tiles_of[last])
-        finish(steps[last], tiles_of[last])
-        store(steps[last], tiles_of[last])
+        kind, jp, r = steps[-1]
+        tiles = tiles_of[len(steps) - 1]
+        features = slice(jp * BLOCK, (jp + 1) * BLOCK)
+        for v in range(UNITS):
+            rows = slice(v * SLOT_PAIR * P, (v + 1) * SLOT_PAIR * P)
+            gate, prop = tiles["gate"], tiles["prop"]
+            nc.scalar.activation(out=gate[:, :, rows], in_=gate[:, :, rows], func=ACT.Sigmoid)
+            nc.vector.tensor_tensor(out=prop[:, :, rows], in0=prop[:, :, rows], in1=gate[:, :, rows], op=ALU.mult)
+        store(steps[-2], tiles_of[len(steps) - 2])
+        for v in range(UNITS):
+            back = back_pool.tile([P, SLOT_PAIR, UNITS, P], F32, tag="back", name="back")
+            for s in range(SLOT_PAIR):
+                for u in range(UNITS):
+                    first_row = (SLOT_PAIR * v + s) * P
+                    nc.tensor.transpose(back[:, s, u, :], prop[:, u, first_row : first_row + P], ident_f[:])
+            pair = slice(v * SLOT_PAIR, (v + 1) * SLOT_PAIR)
+            out_tile = kept[(jp, r)]
+            nc.vector.tensor_tensor(
+                out=out_tile[:, pair, :].rearrange("b s (c u) -> b s c u", u=UNITS),
+                in0=back[:].rearrange("b s u c -> b s c u"),
+                in1=out_tile[:, pair, :].rearrange("b s (c u) -> b s c u", u=UNITS),
+                op=ALU.add,
+            )
+            slots = slice(r * GROUP_SLOTS + v * SLOT_PAIR, r * GROUP_SLOTS + (v + 1) * SLOT_PAIR)
+            nc.sync.dma_start(out=out_0[:, slots, features], in_=out_tile[:, pair, :])

@@ -31,7 +31,7 @@ FLOPS = 2 * P * SLOTS * WIDTH * WIDTH * 4 + 2 * P * WIDTH * WIDTH * 3
 PHASE_WEIGHTS = {"o": ("uo", "wo"), "f": ("uf", "wf"), "ig": ("ui", "wi", "g")}
 BIAS_ORDER = ("g", "f", "i", "o")
 PHASES = [("o", 0), ("o", 1), ("f", 0), ("o", 2), ("f", 1), ("ig", 0), ("o", 3), ("ig", 1), ("f", 2), ("f", 3), ("ig", 2), ("ig", 3)]
-LOADS = [("x", 0), ("wo", "k", 0), ("wo", "k", 1), ("h", 0), ("uo", "k", 0), ("uo", "k", 1), ("h", 1), ("m", 0, 0), ("m", 1, 0), ("uf", "n", 0), ("wf", "n", 0), ("m", 0, 1), ("m", 1, 1), ("p", 0), ("p", 1), ("ui", "n", 0), ("wi", "n", 0), ("g", "n", 0), ("uf", "n", 1), ("wf", "n", 1), ("ui", "n", 1), ("wi", "n", 1), ("g", "n", 1)]
+LOADS = [("x", 0), ("wo", "k", 0), ("wo", "k", 1), ("h", 0), ("uo", "k", 0), ("uo", "k", 1), ("h", 1), ("uf", "n", 0), ("m", 0, 0), ("wf", "n", 0), ("m", 1, 0), ("p", 0), ("p", 1), ("m", 0, 1), ("m", 1, 1), ("ui", "n", 0), ("wi", "n", 0), ("g", "n", 0), ("uf", "n", 1), ("wf", "n", 1), ("ui", "n", 1), ("wi", "n", 1), ("g", "n", 1)]
 TASKS = [("w", "wo", 0, 0), ("w", "wo", 1, 0), ("w", "wo", 2, 0), ("w", "wo", 3, 0), ("w", "wo", 0, 1), ("w", "wo", 1, 1), ("w", "wo", 2, 1), ("w", "wo", 3, 1), ("w", "uo", 0, 0), ("w", "uo", 1, 0), ("w", "uo", 2, 0), ("w", "uo", 3, 0), ("w", "uo", 0, 1), ("w", "uo", 1, 1), ("w", "uo", 2, 1), ("w", "uo", 3, 1), ("w", "uf", 0, 0), ("w", "uf", 0, 1), ("w", "wf", 0, 0), ("w", "wf", 0, 1), ("w", "uf", 1, 0), ("w", "uf", 1, 1), ("w", "wf", 1, 0), ("w", "wf", 1, 1), ("slot", "p", 0, 0), ("slot", "p", 0, 1), ("slot", "p", 0, 2), ("slot", "p", 0, 3), ("slot", "p", 1, 0), ("slot", "p", 1, 1), ("slot", "p", 1, 2), ("slot", "p", 1, 3), ("w", "ui", 0, 0), ("w", "ui", 0, 1), ("w", "wi", 0, 0), ("w", "wi", 0, 1), ("w", "g", 0, 0), ("w", "g", 0, 1), ("w", "ui", 1, 0), ("w", "ui", 1, 1), ("w", "wi", 1, 0), ("w", "wi", 1, 1), ("w", "g", 1, 0), ("w", "g", 1, 1), ("w", "uf", 2, 0), ("w", "uf", 2, 1), ("w", "wf", 2, 0), ("w", "wf", 2, 1), ("w", "uf", 3, 0), ("w", "uf", 3, 1), ("w", "wf", 3, 0), ("w", "wf", 3, 1), ("w", "ui", 2, 0), ("w", "ui", 2, 1), ("w", "wi", 2, 0), ("w", "wi", 2, 1), ("w", "g", 2, 0), ("w", "g", 2, 1), ("w", "ui", 3, 0), ("w", "ui", 3, 1), ("w", "wi", 3, 0), ("w", "wi", 3, 1), ("w", "g", 3, 0), ("w", "g", 3, 1)]
 SHARES = {"o":["VVV","VV"],"f":["VVSS","SVV"],"ig":["S","S"]}
 HEAD = [("w", "wo", 0, 0, "V"), ("w", "wo", 1, 0, "V"), ("w", "wo", 2, 0, "S"), ("w", "wo", 3, 0, "S"), ("w", "wo", 0, 1, "V"), ("q", "wo", 0), ("w", "wo", 1, 1, "V"), ("q", "wo", 1), ("w", "wo", 2, 1, "S"), ("w", "wo", 3, 1, "V"), ("h", 0, "SSSS"), ("q", "wo", 2), ("q", "wo", 3), ("qh", 0), ("w", "uo", 0, 0, "V"), ("w", "uo", 1, 0, "V"), ("w", "uo", 2, 0, "S"), ("w", "uo", 3, 0, "S"), ("mx", 0), ("w", "uo", 0, 1, "V"), ("q", "uo", 0), ("b", 0), ("mh", 0), ("w", "uo", 1, 1, "V"), ("q", "uo", 1), ("h", 1, "SSSS"), ("w", "uo", 2, 1, "V"), ("q", "uo", 2), ("w", "uo", 3, 1, "V"), ("q", "uo", 3), ("qh", 1)]

@@ -185,8 +185,8 @@ def tile_relationalmemorycorecell_pa_kernel(
             copy(out=view[:, :, s, :, :], in_=flipped_of[(name, r, s)])
 
         def quantise_rows(key):
-            codes = const.tile([P, PASSES * ROWS], U32, align_bytes=64, name="codes_%s%d" % key)
-            scales = const.tile([P, PASSES * ROWS], U8, align_bytes=64, name="scales_%s%d" % key)
+            codes = const.tile([P, PASSES * ROWS], U32, align_bytes=256, name="codes_%s%d" % key)
+            scales = const.tile([P, PASSES * ROWS], U8, align_bytes=256, name="scales_%s%d" % key)
             nc.vector.quantize_mx(out=codes[:].bitcast(FP8X4), scales=scales[:], in_=grouped_of[key][:])
             rows_q[key] = (codes, scales)
 
@@ -210,8 +210,8 @@ def tile_relationalmemorycorecell_pa_kernel(
                 load_next_weight()
 
         def quantise_weight(name, jp):
-            codes = w_q_pool.tile([P, PASSES * BLOCK], U32, tag="w_codes", align_bytes=64, name="codes_w")
-            scales = w_q_pool.tile([P, PASSES * BLOCK], U8, tag="w_scales", align_bytes=64, name="scales_w")
+            codes = w_q_pool.tile([P, PASSES * BLOCK], U32, tag="w_codes", align_bytes=256, name="codes_w")
+            scales = w_q_pool.tile([P, PASSES * BLOCK], U8, tag="w_scales", align_bytes=256, name="scales_w")
             nc.vector.quantize_mx(out=codes[:].bitcast(FP8X4), scales=scales[:], in_=grouped_of[(name, jp)][:])
             w_q[(name, jp)] = (codes, scales)
 
@@ -259,7 +259,8 @@ def tile_relationalmemorycorecell_pa_kernel(
                     out=gate[:, u, :], in_=banks[("gate", u)][:], func=ACT.Sigmoid, bias=bias_col(kind[0], jp, u)
                 )
             if kind != "f" and step != steps[-1]:
-                nc.scalar.activation(out=gate[:], in_=gate[:], func=ACT.Sigmoid)
+                for u in range(UNITS):
+                    nc.scalar.activation(out=gate[:, u, :], in_=gate[:, u, :], func=ACT.Sigmoid)
             tiles["gate"] = gate
             if kind == "ig":
                 prop = work.tile([P, UNITS, ROWS], F32, tag="prop", bufs=2, name="prop")
@@ -373,16 +374,16 @@ def tile_relationalmemorycorecell_pa_kernel(
         nc.scalar.copy(
             out=x_grouped[:].bitcast(F32).rearrange("c (g b u) -> c g b u", g=PASSES, b=P, u=2), in_=flip_words(x_sb[:])
         )
-        x_codes = const.tile([P, PASSES, P], U32, align_bytes=64, name="x_codes")
-        x_scales = const.tile([P, PASSES, P], U8, align_bytes=64, name="x_scales")
+        x_codes = const.tile([P, PASSES, P], U32, align_bytes=256, name="x_codes")
+        x_scales = const.tile([P, PASSES, P], U8, align_bytes=256, name="x_scales")
         nc.gpsimd.memset(x_scales[:].rearrange("c g b -> c (g b)").bitcast(I32), 0)
         nc.vector.quantize_mx(
             out=x_codes[:].rearrange("c g b -> c (g b)").bitcast(FP8X4),
             scales=x_scales[:].rearrange("c g b -> c (g b)"),
             in_=x_grouped[:],
         )
-        codes_x = const.tile([P, PASSES * ROWS], U32, align_bytes=64, name="codes_x")
-        scales_x = const.tile([P, PASSES * ROWS], U8, align_bytes=64, name="scales_x")
+        codes_x = const.tile([P, PASSES * ROWS], U32, align_bytes=256, name="codes_x")
+        scales_x = const.tile([P, PASSES * ROWS], U8, align_bytes=256, name="scales_x")
         for many, one, n in ((codes_x, x_codes, P), (scales_x, x_scales, P // 4)):
             nc.vector.tensor_copy(
                 out=many[:].bitcast(I32).rearrange("c (g s n) -> c g s n", g=PASSES, s=GROUP_SLOTS, n=n),

from contextlib import ExitStack

import concourse.mybir as mybir
from concourse.masks import make_identity

F32 = mybir.dt.float32
BF16 = mybir.dt.bfloat16
U32 = mybir.dt.uint32
I32 = mybir.dt.int32
U8 = mybir.dt.uint8
FP8X4 = mybir.dt.float8_e4m3fn_x4
ACT = mybir.ActivationFunctionType
ALU = mybir.AluOpType

P = 128
SLOTS = 8
WIDTH = 1024
PACK = 4
PASSES = WIDTH // (P * PACK)
GROUP_SLOTS = 4
SLOT_PAIR = 2
ROWS = GROUP_SLOTS * P
ROW_GROUPS = SLOTS // GROUP_SLOTS
UNITS = 2
BLOCK = UNITS * P
BLOCKS = WIDTH // BLOCK
HALF = 2 * BLOCK

FLOPS = 2 * P * SLOTS * WIDTH * WIDTH * 4 + 2 * P * WIDTH * WIDTH * 3

PHASE_WEIGHTS = {"o": ("uo", "wo"), "f": ("uf", "wf"), "ig": ("ui", "wi", "g")}
BIAS_ORDER = ("g", "f", "i", "o")
PHASES = [("o", 0), ("o", 1), ("f", 0), ("o", 2), ("f", 1), ("ig", 0), ("o", 3), ("ig", 1), ("f", 2), ("f", 3), ("ig", 2), ("ig", 3)]
LOADS = [("x", 0), ("wo", "k", 0), ("wo", "k", 1), ("h", 0), ("uo", "k", 0), ("uo", "k", 1), ("h", 1), ("uf", "n", 0), ("m", 0, 0), ("wf", "n", 0), ("m", 1, 0), ("p", 0), ("p", 1), ("m", 0, 1), ("m", 1, 1), ("ui", "n", 0), ("wi", "n", 0), ("g", "n", 0), ("uf", "n", 1), ("wf", "n", 1), ("ui", "n", 1), ("wi", "n", 1), ("g", "n", 1)]
TASKS = [("w", "wo", 0, 0), ("w", "wo", 1, 0), ("w", "wo", 2, 0), ("w", "wo", 3, 0), ("w", "wo", 0, 1), ("w", "wo", 1, 1), ("w", "wo", 2, 1), ("w", "wo", 3, 1), ("w", "uo", 0, 0), ("w", "uo", 1, 0), ("w", "uo", 2, 0), ("w", "uo", 3, 0), ("w", "uo", 0, 1), ("w", "uo", 1, 1), ("w", "uo", 2, 1), ("w", "uo", 3, 1), ("w", "uf", 0, 0), ("w", "uf", 0, 1), ("w", "wf", 0, 0), ("w", "wf", 0, 1), ("w", "uf", 1, 0), ("w", "uf", 1, 1), ("w", "wf", 1, 0), ("w", "wf", 1, 1), ("slot", "p", 0, 0), ("slot", "p", 0, 1), ("slot", "p", 0, 2), ("slot", "p", 0, 3), ("slot", "p", 1, 0), ("slot", "p", 1, 1), ("slot", "p", 1, 2), ("slot", "p", 1, 3), ("w", "ui", 0, 0), ("w", "ui", 0, 1), ("w", "wi", 0, 0), ("w", "wi", 0, 1), ("w", "g", 0, 0), ("w", "g", 0, 1), ("w", "ui", 1, 0), ("w", "ui", 1, 1), ("w", "wi", 1, 0), ("w", "wi", 1, 1), ("w", "g", 1, 0), ("w", "g", 1, 1), ("w", "uf", 2, 0), ("w", "uf", 2, 1), ("w", "wf", 2, 0), ("w", "wf", 2, 1), ("w", "uf", 3, 0), ("w", "uf", 3, 1), ("w", "wf", 3, 0), ("w", "wf", 3, 1), ("w", "ui", 2, 0), ("w", "ui", 2, 1), ("w", "wi", 2, 0), ("w", "wi", 2, 1), ("w", "g", 2, 0), ("w", "g", 2, 1), ("w", "ui", 3, 0), ("w", "ui", 3, 1), ("w", "wi", 3, 0), ("w", "wi", 3, 1), ("w", "g", 3, 0), ("w", "g", 3, 1)]
SHARES = {"o":["VVV","VV"],"f":["VVSS","SVV"],"ig":["S","S"]}
HEAD = [("w", "wo", 0, 0, "V"), ("w", "wo", 1, 0, "V"), ("w", "wo", 2, 0, "S"), ("w", "wo", 3, 0, "S"), ("w", "wo", 0, 1, "V"), ("q", "wo", 0), ("w", "wo", 1, 1, "V"), ("q", "wo", 1), ("w", "wo", 2, 1, "S"), ("w", "wo", 3, 1, "V"), ("h", 0, "SSSS"), ("q", "wo", 2), ("q", "wo", 3), ("qh", 0), ("w", "uo", 0, 0, "V"), ("w", "uo", 1, 0, "V"), ("w", "uo", 2, 0, "S"), ("w", "uo", 3, 0, "S"), ("mx", 0), ("w", "uo", 0, 1, "V"), ("q", "uo", 0), ("b", 0), ("mh", 0), ("w", "uo", 1, 1, "V"), ("q", "uo", 1), ("h", 1, "SSSS"), ("w", "uo", 2, 1, "V"), ("q", "uo", 2), ("w", "uo", 3, 1, "V"), ("q", "uo", 3), ("qh", 1)]
W_RAW_BUFS = 5
W_Q_BUFS = 12
GROUPED_BUFS = 5
OUT_BUFS = {"o":3,"f":6}
ACC_BUFS = 4
TANH_EARLY = False
FINISH_LATE = True
MULT_FIRST = {"o": True, "f": True, "ig": False}
TASKS_FIRST = {"o": True, "f": True, "ig": False}
PINNED = {mybir.EngineType.PE, mybir.EngineType.DVE, mybir.EngineType.Activation}


def tile_relationalmemorycorecell_pa_kernel(
    tc, inputs, h_state, m_state, mem_att, W_g, b_g, W_wf, W_wi, W_wo, W_uf, b_uf, W_ui, b_ui, W_uo, b_uo, out_0, out_1
):
    nc = tc.nc
    weight_of = {"g": W_g, "wf": W_wf, "wi": W_wi, "wo": W_wo, "uf": W_uf, "ui": W_ui, "uo": W_uo}
    bias_of = {"g": b_g, "f": b_uf, "i": b_ui, "o": b_uo}
    rows_of = {"h": h_state, "p": mem_att}
    steps = [(kind, jp, r) for (kind, jp) in PHASES for r in range(ROW_GROUPS)]
    SC, VC = nc.scalar.copy, nc.vector.tensor_copy

    def gpsimd_copy(out, in_):
        nc.gpsimd.tensor_scalar(out=out, in0=in_, scalar1=1.0, scalar2=0.0, op0=ALU.mult, op1=ALU.add)

    COPY = {"S": SC, "V": VC, "G": gpsimd_copy, "P": SC}

    with ExitStack() as ctx:
        const = ctx.enter_context(tc.tile_pool(name="const", bufs=1))
        rows_pool = ctx.enter_context(tc.tile_pool(name="rows", bufs=2))
        w_raw_pool = ctx.enter_context(tc.tile_pool(name="w_raw", bufs=W_RAW_BUFS))
        w_grouped_pool = ctx.enter_context(tc.tile_pool(name="w_grouped", bufs=GROUPED_BUFS))
        w_q_pool = ctx.enter_context(tc.tile_pool(name="w_q", bufs=W_Q_BUFS))
        work = ctx.enter_context(tc.tile_pool(name="work", bufs=3))
        acc_pool = ctx.enter_context(tc.psum_pool(name="acc", bufs=ACC_BUFS))
        back_pool = ctx.enter_context(tc.psum_pool(name="back", bufs=8 - ACC_BUFS))

        ident_f = const.tile([P, P], F32, name="ident_f")
        make_identity(nc, ident_f[:])

        x_sb = const.tile([P, WIDTH], BF16, name="x_sb")
        rows_raw = {}
        m_rows = {}
        w_raw = {}
        readers_left = {}
        chunk_of = {}

        def load_rows(name, r):
            raw = rows_pool.tile([P, GROUP_SLOTS * WIDTH], BF16, tag="rows_raw", name="raw_" + name)
            src = rows_of[name][:, r * GROUP_SLOTS : (r + 1) * GROUP_SLOTS, :]
            if name == "h":
                for s in range(GROUP_SLOTS):
                    nc.sync.dma_start(out=raw[:, s * WIDTH : (s + 1) * WIDTH], in_=src[:, s, :])
            else:
                nc.sync.dma_start(out=raw[:], in_=src.rearrange("b s n -> b (s n)"))
            rows_raw[(name, r)] = raw

        def load_m(r, half):
            m_rows[(r, half)] = const.tile([P, GROUP_SLOTS, HALF], BF16, name="m_rows%d%d" % (r, half))
            nc.sync.dma_start(
                out=m_rows[(r, half)][:],
                in_=m_state[:, r * GROUP_SLOTS : (r + 1) * GROUP_SLOTS, half * HALF : (half + 1) * HALF],
            )

        def m_block(jp, r):
            return m_rows[(r, jp // 2)][:, :, jp % 2 * BLOCK : (jp % 2 + 1) * BLOCK]

        def load_weight(name, how, k):
            raw = w_raw_pool.tile([P, 2 * PACK * HALF], BF16, tag="w_raw", name="raw_" + name)
            readers_left[(name, how, k)] = 4
            if how == "n":
                dst = raw[:].rearrange("c (a e n) -> c a e n", e=2, n=HALF)
                src = weight_of[name][:, k * HALF : (k + 1) * HALF].rearrange("(a c e) n -> c a e n", c=P, e=2)
                for e in range(2):
                    nc.sync.dma_start(out=dst[:, :, e, :], in_=src[:, :, e, :])
                words = raw[:].rearrange("c (g t n) -> c g t n", g=PASSES, t=PACK)
                for g in range(PASSES):
                    w_raw[(name, k, g)] = words[:, g]
                    chunk_of[(name, k, g)] = (name, how, k)
            else:
                src = weight_of[name][k * P * PACK : (k + 1) * P * PACK, :]
                nc.sync.dma_start(
                    out=raw[:].rearrange("c (u m) -> c u m", u=2), in_=src.rearrange("(u c e) n -> c u (e n)", c=P, e=2)
                )
                words = raw[:].rearrange("c (t n) -> c t n", t=PACK)
                for half in range(2):
                    w_raw[(name, half, k)] = words[:, :, half * HALF : (half + 1) * HALF]
                    chunk_of[(name, half, k)] = (name, how, k)

        loads = list(LOADS)

        def load_next_weight():
            seen = False
            while loads and not (seen and loads[0][0] in weight_of):
                load = loads.pop(0)
                seen = seen or load[0] in weight_of
                if load[0] in weight_of:
                    load_weight(load[0], load[1], load[2])
                elif load[0] == "m":
                    load_m(load[1], load[2])
                elif load[0] == "x":
                    nc.sync.dma_start(out=x_sb[:], in_=inputs)
                else:
                    load_rows(load[0], load[1])

        for count in range(W_RAW_BUFS):
            load_next_weight()

        bias_rows = const.tile([P, BLOCK], BF16, name="bias_rows")
        nc.vector.memset(bias_rows[:], 0.0)
        for k, key in enumerate(BIAS_ORDER):
            nc.scalar.dma_start(
                out=bias_rows[k * BLOCKS : (k + 1) * BLOCKS, :],
                in_=bias_of[key].rearrange("(j n) -> j n", n=BLOCK),
            )
        bias_cols = const.tile([P, P], F32, name="bias_cols")

        def bias_col(key, jp, u):
            col = (BIAS_ORDER.index(key) * BLOCKS + jp) * UNITS + u
            return bias_cols[:, col : col + 1]

        rows_q = {}
        w_q = {}
        grouped_of = {}

        def flip_words(raw_cols):
            flipped = back_pool.tile([P, WIDTH // 2], F32, tag="back", name="flipped_words")
            words = raw_cols.bitcast(F32)
            for a in range(WIDTH // 2 // P):
                nc.tensor.transpose(flipped[:, a * P : (a + 1) * P], words[:, a * P : (a + 1) * P], ident_f[:])
            return flipped[:].rearrange("c (g u b) -> c g b u", g=PASSES, u=2, b=P)

        flipped_of = {}

        def flip_slot(name, r, s):
            flipped_of[(name, r, s)] = flip_words(rows_raw[(name, r)][:, s * WIDTH : (s + 1) * WIDTH])

        def group_slot(name, r, s, copy):
            if (name, r) not in grouped_of:
                grouped_of[(name, r)] = rows_pool.tile(
                    [P, PASSES * ROWS * PACK], BF16, tag="rows_grouped", align_bytes=64, name="grouped_" + name
                )
            view = grouped_of[(name, r)][:].bitcast(F32).rearrange(
                "c (g s b u) -> c g s b u", g=PASSES, s=GROUP_SLOTS, b=P, u=2
            )
            if (name, r, s) not in flipped_of:
                flip_slot(name, r, s)
            copy(out=view[:, :, s, :, :], in_=flipped_of[(name, r, s)])

        def quantise_rows(key):
            codes = const.tile([P, PASSES * ROWS], U32, align_bytes=256, name="codes_%s%d" % key)
            scales = const.tile([P, PASSES * ROWS], U8, align_bytes=256, name="scales_%s%d" % key)
            nc.vector.quantize_mx(out=codes[:].bitcast(FP8X4), scales=scales[:], in_=grouped_of[key][:])
            rows_q[key] = (codes, scales)

        def raw_block(name, jp, g):
            return w_raw[(name, jp // 2, g)][:, :, jp % 2 * BLOCK : (jp % 2 + 1) * BLOCK]

        def group_weight(name, jp, g, copy):
            key = (name, jp)
            if key not in grouped_of:
                grouped_of[key] = w_grouped_pool.tile(
                    [P, PASSES * BLOCK * PACK], BF16, tag="w_grouped", align_bytes=64, name="grouped_w"
                )
            dst = grouped_of[key][:, g * BLOCK * PACK : (g + 1) * BLOCK * PACK]
            copy(
                out=dst.rearrange("c (u n i t) -> c n t i u", u=UNITS, i=2, t=PACK),
                in_=raw_block(name, jp, g).rearrange("c t (n i u) -> c n t i u", u=UNITS, i=2),
            )
            chunk = chunk_of[(name, jp // 2, g)]
            readers_left[chunk] = readers_left[chunk] - 1
            if readers_left[chunk] == 0:
                load_next_weight()

        def quantise_weight(name, jp):
            codes = w_q_pool.tile([P, PASSES * BLOCK], U32, tag="w_codes", align_bytes=256, name="codes_w")
            scales = w_q_pool.tile([P, PASSES * BLOCK], U8, tag="w_scales", align_bytes=256, name="scales_w")
            nc.vector.quantize_mx(out=codes[:].bitcast(FP8X4), scales=scales[:], in_=grouped_of[(name, jp)][:])
            w_q[(name, jp)] = (codes, scales)

        def add_passes(acc, name, jp, u, moving_q, first, last):
            r_codes, r_scales = moving_q
            for g in range(PASSES):
                w_codes, w_scales = w_q[(name, jp)]
                m_cols = slice(g * BLOCK + u * P, g * BLOCK + (u + 1) * P)
                n_cols = slice(g * ROWS, (g + 1) * ROWS)
                nc.tensor.matmul_mx(
                    out=acc[:],
                    lhsT=w_codes[:, m_cols].bitcast(FP8X4),
                    lhsT_scale=w_scales[:, m_cols],
                    rhs=r_codes[:, n_cols].bitcast(FP8X4),
                    rhs_scale=r_scales[:, n_cols],
                    start=(first and g == 0),
                    stop=(last and g == PASSES - 1),
                )

        def multiply_inputs(step):
            kind, jp, r = step
            banks = {}
            for u in range(UNITS):
                acc = acc_pool.tile([P, ROWS], F32, tag="acc", name="acc_gate")
                add_passes(acc, PHASE_WEIGHTS[kind][1], jp, u, rows_q[("x", 0)], True, False)
                banks[("gate", u)] = acc
            return banks

        def multiply_rows(step, banks):
            kind, jp, r = step
            for u in range(UNITS):
                add_passes(banks[("gate", u)], PHASE_WEIGHTS[kind][0], jp, u, rows_q[("h", r)], False, True)
            if kind == "ig":
                for u in range(UNITS):
                    acc = acc_pool.tile([P, ROWS], F32, tag="acc", name="acc_prop")
                    add_passes(acc, "g", jp, u, rows_q[("p", r)], True, True)
                    banks[("prop", u)] = acc

        def activate(step, banks):
            kind, jp, r = step
            tiles = {}
            gate = work.tile([P, UNITS, ROWS], F32, tag="gate", name="gate")
            for u in range(UNITS):
                nc.scalar.activation(
                    out=gate[:, u, :], in_=banks[("gate", u)][:], func=ACT.Sigmoid, bias=bias_col(kind[0], jp, u)
                )
            if kind != "f" and step != steps[-1]:
                for u in range(UNITS):
                    nc.scalar.activation(out=gate[:, u, :], in_=gate[:, u, :], func=ACT.Sigmoid)
            tiles["gate"] = gate
            if kind == "ig":
                prop = work.tile([P, UNITS, ROWS], F32, tag="prop", bufs=2, name="prop")
                p_view = grouped_of[("p", r)][:].rearrange("c (g w t) -> c g w t", g=PASSES, w=ROWS, t=PACK)
                for u in range(UNITS):
                    nc.vector.scalar_tensor_tensor(
                        out=prop[:, u, :],
                        in0=banks[("prop", u)][:],
                        scalar=bias_col("g", jp, u),
                        in1=p_view[:, jp // UNITS, :, jp % UNITS * UNITS + u],
                        op0=ALU.add,
                        op1=ALU.add,
                    )
                tiles["prop"] = prop
            return tiles

        def squash(step, tiles):
            kind, jp, r = step
            if kind == "o":
                tanh_m = work.tile([P, GROUP_SLOTS, BLOCK], F32, tag="tanh", bufs=2, name="tanh_m")
                nc.scalar.activation(out=tanh_m[:], in_=m_block(jp, r), func=ACT.Tanh)
                tiles["tanh"] = tanh_m

        def weigh(step, tiles):
            if step[0] == "ig" and step != steps[-1]:
                prop = tiles["prop"]
                nc.vector.tensor_tensor(out=prop[:], in0=prop[:], in1=tiles["gate"][:], op=ALU.mult)

        def flip_back(step, tiles):
            result = tiles["prop" if step[0] == "ig" else "gate"]
            for v in range(UNITS):
                back = back_pool.tile([P, SLOT_PAIR, UNITS, P], F32, tag="back", name="back")
                for s in range(SLOT_PAIR):
                    rows = slice((SLOT_PAIR * v + s) * P, (SLOT_PAIR * v + s + 1) * P)
                    for u in range(UNITS):
                        nc.tensor.transpose(back[:, s, u, :], result[:, u, rows], ident_f[:])
                tiles[("back", v)] = back

        kept = {}

        def combine(step, tiles):
            kind, jp, r = step
            features = slice(jp * BLOCK, (jp + 1) * BLOCK)
            if kind == "ig":
                out_tile = kept[(jp, r)]
            else:
                out_tile = work.tile([P, GROUP_SLOTS, BLOCK], F32, tag="out_" + kind, bufs=OUT_BUFS[kind], name="out_" + kind)
            for v in range(UNITS):
                pair = slice(v * SLOT_PAIR, (v + 1) * SLOT_PAIR)
                other = {"o": tiles.get("tanh"), "f": m_block(jp, r), "ig": out_tile}[kind]
                nc.vector.tensor_tensor(
                    out=out_tile[:, pair, :].rearrange("b s (c u) -> b s c u", u=UNITS),
                    in0=tiles[("back", v)][:].rearrange("b s u c -> b s c u"),
                    in1=other[:, pair, :].rearrange("b s (c u) -> b s c u", u=UNITS),
                    op=(ALU.add if kind == "ig" else ALU.mult),
                )
            tiles["out"] = out_tile

        def finish(step, tiles):
            kind, jp, r = step
            if kind == "f":
                nc.scalar.activation(out=tiles["out"][:], in_=tiles["out"][:], func=ACT.Sigmoid, bias=1.0)
                kept[(jp, r)] = tiles["out"]

        def store(step, tiles):
            kind, jp, r = step
            slots = slice(r * GROUP_SLOTS, (r + 1) * GROUP_SLOTS)
            features = slice(jp * BLOCK, (jp + 1) * BLOCK)
            if kind == "o":
                nc.scalar.dma_start(out=out_1[:, slots, features], in_=tiles["out"][:])
            if kind == "ig":
                nc.scalar.dma_start(out=out_0[:, slots, features], in_=tiles["out"][:])

        tasks = list(TASKS)
        halves_done = {}
        waiting = []

        def run_tasks(engines):
            for letter in engines:
                if not tasks:
                    return
                task = tasks.pop(0)
                if task[0] == "slot":
                    group_slot(task[1], task[2], task[3], SC if letter in "SP" else VC)
                    if task[3] == GROUP_SLOTS - 1:
                        waiting.append(task)
                else:
                    group_weight(task[1], task[2], task[3], COPY[letter])
                    halves_done[(task[1], task[2])] = halves_done.get((task[1], task[2]), 0) + 1
                    if halves_done[(task[1], task[2])] == PASSES:
                        waiting.append(task)

        def run_quantises():
            while waiting:
                task = waiting.pop(0)
                if task[0] == "slot":
                    quantise_rows((task[1], task[2]))
                else:
                    quantise_weight(task[1], task[2])

        def ensure(step):
            kind, jp, r = step
            need = [(n, jp) for n in PHASE_WEIGHTS[kind]]
            while any([k not in w_q for k in need]) or (kind == "ig" and ("p", r) not in rows_q):
                if not waiting:
                    run_tasks("V")
                run_quantises()

        ctx.enter_context(tc.manual_schedule(engines=PINNED))
        x_grouped = const.tile([P, WIDTH], BF16, align_bytes=64, name="grouped_x")
        nc.scalar.copy(
            out=x_grouped[:].bitcast(F32).rearrange("c (g b u) -> c g b u", g=PASSES, b=P, u=2), in_=flip_words(x_sb[:])
        )
        x_codes = const.tile([P, PASSES, P], U32, align_bytes=256, name="x_codes")
        x_scales = const.tile([P, PASSES, P], U8, align_bytes=256, name="x_scales")
        nc.gpsimd.memset(x_scales[:].rearrange("c g b -> c (g b)").bitcast(I32), 0)
        nc.vector.quantize_mx(
            out=x_codes[:].rearrange("c g b -> c (g b)").bitcast(FP8X4),
            scales=x_scales[:].rearrange("c g b -> c (g b)"),
            in_=x_grouped[:],
        )
        codes_x = const.tile([P, PASSES * ROWS], U32, align_bytes=256, name="codes_x")
        scales_x = const.tile([P, PASSES * ROWS], U8, align_bytes=256, name="scales_x")
        for many, one, n in ((codes_x, x_codes, P), (scales_x, x_scales, P // 4)):
            nc.vector.tensor_copy(
                out=many[:].bitcast(I32).rearrange("c (g s n) -> c g s n", g=PASSES, s=GROUP_SLOTS, n=n),
                in_=one[:].bitcast(I32).unsqueeze(2).to_broadcast([P, PASSES, GROUP_SLOTS, n]),
            )
        rows_q[("x", 0)] = (codes_x, scales_x)
        banks = {}
        for op in HEAD:
            if op[0] == "w":
                group_weight(op[1], op[2], op[3], COPY[op[4]])
                tasks.remove(("w", op[1], op[2], op[3]))
                halves_done[(op[1], op[2])] = halves_done.get((op[1], op[2]), 0) + 1
            elif op[0] == "q":
                quantise_weight(op[1], op[2])
            elif op[0] == "h":
                for s in range(GROUP_SLOTS):
                    group_slot("h", op[1], s, COPY[op[2][s]])
            elif op[0] == "qh":
                quantise_rows(("h", op[1]))
            elif op[0] == "mx":
                banks = multiply_inputs(steps[0])
            elif op[0] == "mh":
                multiply_rows(steps[0], banks)
            elif op[0] == "b":
                bias_flipped = back_pool.tile([P, P], F32, tag="back", name="bias_flipped")
                nc.tensor.transpose(bias_flipped[:], bias_rows[:].bitcast(F32), ident_f[:])
                n_bias = len(BIAS_ORDER) * BLOCKS * UNITS
                nc.vector.tensor_copy(out=bias_cols[:, 0:n_bias], in_=bias_flipped[:].bitcast(BF16)[:, 0:n_bias])

        tiles_of = {}

        def share_of(i):
            shares = SHARES[steps[i][0]]
            return shares[i % len(shares)]

        def do_multiply(i):
            if i + 1 < len(steps):
                ensure(steps[i + 1])
                banks = multiply_inputs(steps[i + 1])
                multiply_rows(steps[i + 1], banks)
                return banks
            return {}

        def do_tasks(i):
            run_quantises()
            run_tasks(share_of(i))

        for i, step in enumerate(steps):
            tiles_of[i] = activate(step, banks)
            pe_first = "A" if MULT_FIRST[step[0]] else "D"
            if pe_first == "A":
                banks = do_multiply(i)
            if i >= 1:
                flip_back(steps[i - 1], tiles_of[i - 1])
            if pe_first == "D":
                banks = do_multiply(i)
            if i + 1 < len(steps):
                ahead = len(share_of(i))
                for task in tasks[ahead : ahead + len(share_of(i + 1))]:
                    if task[0] == "slot":
                        flip_slot(task[1], task[2], task[3])
            if FINISH_LATE and i >= 2:
                finish(steps[i - 2], tiles_of[i - 2])
            if TANH_EARLY:
                squash(step, tiles_of[i])
            if TASKS_FIRST[step[0]]:
                do_tasks(i)
            if i >= 1:
                combine(steps[i - 1], tiles_of[i - 1])
            if not FINISH_LATE and i >= 1:
                finish(steps[i - 1], tiles_of[i - 1])
            if not TASKS_FIRST[step[0]]:
                do_tasks(i)
            if not TANH_EARLY:
                squash(step, tiles_of[i])
            if FINISH_LATE and i >= 2:
                store(steps[i - 2], tiles_of[i - 2])
            if not FINISH_LATE and i >= 1:
                store(steps[i - 1], tiles_of[i - 1])
            weigh(step, tiles_of[i])
        kind, jp, r = steps[-1]
        tiles = tiles_of[len(steps) - 1]
        features = slice(jp * BLOCK, (jp + 1) * BLOCK)
        for v in range(UNITS):
            rows = slice(v * SLOT_PAIR * P, (v + 1) * SLOT_PAIR * P)
            gate, prop = tiles["gate"], tiles["prop"]
            nc.scalar.activation(out=gate[:, :, rows], in_=gate[:, :, rows], func=ACT.Sigmoid)
            nc.vector.tensor_tensor(out=prop[:, :, rows], in0=prop[:, :, rows], in1=gate[:, :, rows], op=ALU.mult)
        store(steps[-2], tiles_of[len(steps) - 2])
        for v in range(UNITS):
            back = back_pool.tile([P, SLOT_PAIR, UNITS, P], F32, tag="back", name="back")
            for s in range(SLOT_PAIR):
                for u in range(UNITS):
                    first_row = (SLOT_PAIR * v + s) * P
                    nc.tensor.transpose(back[:, s, u, :], prop[:, u, first_row : first_row + P], ident_f[:])
            pair = slice(v * SLOT_PAIR, (v + 1) * SLOT_PAIR)
            out_tile = kept[(jp, r)]
            nc.vector.tensor_tensor(
                out=out_tile[:, pair, :].rearrange("b s (c u) -> b s c u", u=UNITS),
                in0=back[:].rearrange("b s u c -> b s c u"),
                in1=out_tile[:, pair, :].rearrange("b s (c u) -> b s c u", u=UNITS),
                op=ALU.add,
            )
            slots = slice(r * GROUP_SLOTS + v * SLOT_PAIR, r * GROUP_SLOTS + (v + 1) * SLOT_PAIR)
            nc.sync.dma_start(out=out_0[:, slots, features], in_=out_tile[:, pair, :])
